import numpy as np
import ml_dtypes


def mxq(x, axis, fmt="e4m3"):
    dtype, down = {"e4m3": (ml_dtypes.float8_e4m3fn, 7), "e5m2": (ml_dtypes.float8_e5m2, 14)}[fmt]
    v = np.moveaxis(np.asarray(x, np.float32).astype(ml_dtypes.bfloat16).astype(np.float64), axis, -1)
    blocks = v.reshape(v.shape[:-1] + (-1, 32))
    amax = np.abs(blocks).max(-1, keepdims=True)
    byte = np.maximum(np.where(amax > 0, np.frexp(amax)[1] - 1 + 127, 0) - down, 1)
    scale = np.exp2(byte - 127.0)
    codes = (blocks / scale).astype(np.float32).astype(dtype).astype(np.float64)
    return np.moveaxis((codes * scale).reshape(v.shape), -1, axis)


WIDE = False


def mx_kscale(k):
    if not WIDE:
        return np.ones(k)
    levels = np.array([10, -10, 5, -5, 0])
    a = np.random.permutation(np.resize(levels, k // 512 * 4)).reshape(k // 512, 4)
    idx = np.arange(k)
    return np.exp2(a[idx // 512, idx % 128 // 32])


BF16 = ml_dtypes.bfloat16


def bf(x):
    return np.asarray(x, np.float32).astype(BF16)


def f64(x):
    return np.asarray(x).astype(np.float64)


B, T, D, M, C = 1, 1024, 512, 4, 512
MD = M * D
LN_EPS = 1e-5


def setup_inputs():
    s, t = mx_kscale(T), mx_kscale(MD)
    sc = np.random.standard_normal((B, M, T, T)) * 2.0
    sc = np.where(np.tril(np.ones((T, T), dtype=bool)), sc, -np.inf)
    e = np.exp(sc - sc.max(-1, keepdims=True))
    attn = e / e.sum(-1, keepdims=True)
    return {"attn": bf(attn * s),
            "pz": bf(np.random.standard_normal((B, M, T, D)) / s[:, None] * t.reshape(M, 1, D)),
            "Wo": bf(np.random.standard_normal((D, MD)) * 2.0 / np.sqrt(MD) / t),
            "bo": bf(np.random.standard_normal(D) * 0.3),
            "x": bf(np.random.standard_normal((B, T, D))),
            "gamma": bf(1.0 + 0.1 * np.random.standard_normal(D)),
            "beta": bf(0.1 * np.random.standard_normal(D))}


def reference(attn, pz, Wo, bo, x, gamma, beta):
    a = f64(attn)
    pq = mxq(f64(pz), 2, "e4m3")
    rows = []
    for r in range(0, T, C):
        aq = mxq(a[:, :, r:r + C, :r + C], 3, "e4m3")
        rows.append(aq @ pq[:, :, :r + C, :])
    out = np.concatenate(rows, axis=2)
    cat = out.transpose(0, 2, 1, 3).reshape(B, T, MD)
    y = (mxq(cat, 2, "e4m3") @ mxq(f64(Wo), 1, "e4m3").T) + f64(bo)
    h = y + f64(x)
    mu = h.mean(-1, keepdims=True)
    var = h.var(-1, keepdims=True)
    return (h - mu) / np.sqrt(var + LN_EPS) * f64(gamma) + f64(beta)

@@ -1,0 +1,359 @@
+from contextlib import ExitStack
+
+import concourse.mybir as mybir
+from concourse.masks import make_identity
+
+F32 = mybir.dt.float32
+BF16 = mybir.dt.bfloat16
+U32 = mybir.dt.uint32
+U8 = mybir.dt.uint8
+FP8X4 = mybir.dt.float8_e4m3fn_x4
+ALU = mybir.AluOpType
+ACT = mybir.ActivationFunctionType
+
+P = 128
+PACK = 4
+K_PASS = P * PACK
+HALF_PASS = K_PASS // 2
+HEADS = 4
+T = 1024
+D = 512
+TILES = T // P
+CAUSAL_BLOCK = 512
+LN_EPS = 1e-5
+
+FLOPS = 2 * HEADS * D * (CAUSAL_BLOCK * CAUSAL_BLOCK + CAUSAL_BLOCK * T) + 2 * T * HEADS * D * D
+BYTES = 2 * (HEADS * T * (T + 1) // 2 + HEADS * T * D + D * HEADS * D + T * D + 3 * D) + 4 * T * D
+
+
+def key_passes(j):
+    return (j * P) // CAUSAL_BLOCK + 1
+
+
+def tile_softmaxattention_pb_kernel(tc, attn, pz, Wo, bo, x, gamma, beta, out):
+    nc = tc.nc
+    with ExitStack() as ctx:
+        inputs = ctx.enter_context(tc.tile_pool(name="inputs", bufs=1))
+        const = ctx.enter_context(tc.tile_pool(name="const", bufs=1))
+        weights = ctx.enter_context(tc.tile_pool(name="weights", bufs=1))
+        stage = ctx.enter_context(tc.tile_pool(name="stage", bufs=2))
+        stats = ctx.enter_context(tc.tile_pool(name="stats", bufs=3))
+        psum_t = ctx.enter_context(tc.psum_pool(name="psum_t", bufs=3))
+        psum_cat = ctx.enter_context(tc.psum_pool(name="psum_cat", bufs=HEADS))
+        psum_y = ctx.enter_context(tc.psum_pool(name="psum_y", bufs=1))
+
+        pz_raw = [
+            [inputs.tile([P, PACK, D], BF16, name="pz_raw_%d_%d" % (m, g)) for g in range(2)]
+            for m in range(HEADS)
+        ]
+        wo_raw = [inputs.tile([P, PACK, K_PASS], BF16, name="wo_raw_%d" % m) for m in range(HEADS)]
+        attn_raw = [
+            inputs.tile([P, HEADS, key_passes(j) * K_PASS], BF16, name="attn_raw_%d" % j)
+            for j in range(TILES)
+        ]
+        x_sb = inputs.tile([P, TILES, D], BF16)
+
+        def load_pz(m, g):
+            nc.sync.dma_start(
+                out=pz_raw[m][g][:].rearrange("p (u e) i -> p u (e i)", u=2),
+                in_=pz[0, m, g * K_PASS : (g + 1) * K_PASS, :].rearrange(
+                    "(u p e) i -> p u (e i)", u=2, e=2
+                ),
+            )
+
+        def load_wo(m):
+            nc.sync.dma_start(
+                out=wo_raw[m][:],
+                in_=Wo[:, m * K_PASS : (m + 1) * K_PASS].rearrange("(r q) c -> q r c", q=P),
+            )
+
+        def load_attn(j):
+            keys = key_passes(j) * K_PASS
+            nc.sync.dma_start(
+                out=attn_raw[j][:],
+                in_=attn[0, :, j * P : (j + 1) * P, 0:keys].rearrange("m p s -> p m s"),
+            )
+
+        def load_x(half):
+            tiles = slice(half * TILES // 2, (half + 1) * TILES // 2)
+            rows = slice(half * T // 2, (half + 1) * T // 2)
+            nc.sync.dma_start(
+                out=x_sb[:, tiles, :], in_=x[0, rows, :].rearrange("(j p) o -> p j o", p=P)
+            )
+
+        load_pz(0, 0)
+        load_attn(0)
+        load_wo(0)
+        for m in range(1, HEADS):
+            load_pz(m, 0)
+            load_wo(m)
+        load_attn(1)
+        load_attn(2)
+        load_pz(0, 1)
+        load_x(0)
+        for m in range(1, HEADS):
+            load_attn(2 + m)
+            load_pz(m, 1)
+        load_attn(6)
+        load_attn(7)
+        load_x(1)
+
+        ident_f32 = const.tile([P, P], F32)
+        make_identity(nc, ident_f32[:])
+        ident_bf16 = const.tile([P, P], BF16)
+        make_identity(nc, ident_bf16[:])
+        ones = const.tile([P, P], BF16)
+        nc.vector.memset(ones[:], 1.0)
+        eps_col = const.tile([P, 1], F32)
+        nc.vector.memset(eps_col[:], LN_EPS)
+
+        vec_loaded = const.tile([1, 3, D], BF16)
+        for k, vec in enumerate((bo, gamma, beta)):
+            nc.scalar.dma_start(out=vec_loaded[0:1, k, :], in_=vec.rearrange("(o n) -> o n", o=1))
+        vec_rows = const.tile([P, 3, D], BF16)
+        nc.vector.memset(vec_rows[:], 0.0)
+        nc.vector.tensor_copy(out=vec_rows[0:1, :, :], in_=vec_loaded[:])
+        spread = []
+        warm = const.tile([P, 1], F32)
+        nc.scalar.activation(out=warm[:], in_=eps_col[:], func=ACT.Sqrt)
+        for k in range(3):
+            vec_ps = psum_t.tile([P, D], F32, tag="tp")
+            nc.tensor.matmul(out=vec_ps[:], lhsT=ones[:], rhs=vec_rows[:, k, :], start=True, stop=True)
+            vec_bc = const.tile([P, D], F32, name="vec_bc_%d" % k)
+            nc.scalar.copy(out=vec_bc[:], in_=vec_ps[:])
+            spread.append(vec_bc)
+        bo_bc, gamma_bc, beta_bc = spread
+
+        pz_codes = [
+            [weights.tile([P, D], U32, name="pz_codes_%d_%d" % (m, g), align_bytes=64) for g in range(2)]
+            for m in range(HEADS)
+        ]
+        pz_scales = [
+            [weights.tile([P, D], U8, name="pz_scales_%d_%d" % (m, g), align_bytes=64) for g in range(2)]
+            for m in range(HEADS)
+        ]
+        wo_codes = [weights.tile([P, D], U32, name="wo_codes_%d" % m, align_bytes=64) for m in range(HEADS)]
+        wo_scales = [weights.tile([P, D], U8, name="wo_scales_%d" % m, align_bytes=64) for m in range(HEADS)]
+        pz_grouped = {}
+        wo_grouped = {}
+
+        def regroup_pz(m, g):
+            grouped = stage.tile([P, D, PACK], BF16, tag="w_grouped", bufs=3, align_bytes=64)
+            nc.vector.tensor_copy(
+                out=grouped[:].rearrange("p (c i) k -> p c k i", i=4),
+                in_=pz_raw[m][g][:].rearrange("p k (c i) -> p c k i", i=4),
+            )
+            pz_grouped[(m, g)] = grouped
+
+        def quantise_pz(m, g):
+            nc.vector.quantize_mx(
+                out=pz_codes[m][g][:].bitcast(FP8X4),
+                scales=pz_scales[m][g][:],
+                in_=pz_grouped[(m, g)][:].rearrange("p i k -> p (i k)"),
+            )
+
+        def transpose_wo(m):
+            grouped = stage.tile([P, D, PACK], BF16, tag="w_grouped", bufs=3, align_bytes=64)
+            for half in range(2):
+                wo_t = psum_t.tile([P, 2, PACK, P], BF16, tag="tp")
+                for r in range(2):
+                    for a in range(PACK):
+                        nc.tensor.transpose(
+                            wo_t[:, r, a, :],
+                            wo_raw[m][:, 2 * half + r, a * P : (a + 1) * P],
+                            ident_bf16[:],
+                        )
+                nc.scalar.copy(
+                    out=grouped[:, 2 * half * P : 2 * (half + 1) * P, :].rearrange(
+                        "p (r q) a -> p r q a", r=2
+                    ),
+                    in_=wo_t[:].rearrange("p r a q -> p r q a"),
+                )
+            wo_grouped[m] = grouped
+
+        def quantise_wo(m):
+            nc.vector.quantize_mx(
+                out=wo_codes[m][:].bitcast(FP8X4),
+                scales=wo_scales[m][:],
+                in_=wo_grouped[m][:].rearrange("p o a -> p (o a)"),
+            )
+
+        att_grouped = {}
+        att_q = {}
+        cat_grouped = {}
+        cat_q = {}
+        y_ps = {}
+        xb = {}
+        h = {}
+        negmean = {}
+        std = {}
+        centred = {}
+
+        def transpose_attn(j):
+            passes = key_passes(j)
+            units = HEADS * passes
+            grouped = stage.tile([P, units * K_PASS], BF16, tag="att_grouped", align_bytes=64)
+            words = grouped[:].bitcast(F32).rearrange("p (n t u) -> p n t u", t=P, u=2)
+            for b in range(units // 2):
+                att_t = psum_t.tile([P, 2, 2, P], F32, tag="tp")
+                for n in range(2):
+                    m, g = divmod(2 * b + n, passes)
+                    for u in range(2):
+                        k0 = g * K_PASS + u * HALF_PASS
+                        nc.tensor.transpose(
+                            att_t[:, n, u, :],
+                            attn_raw[j][:, m, k0 : k0 + HALF_PASS].bitcast(F32),
+                            ident_f32[:],
+                        )
+                nc.scalar.copy(
+                    out=words[:, 2 * b : 2 * b + 2, :, :], in_=att_t[:].rearrange("p n u t -> p n t u")
+                )
+            att_grouped[j] = grouped
+
+        def quantise_attn(j):
+            units = HEADS * key_passes(j)
+            codes = stage.tile([P, units, P], U32, tag="att_codes", align_bytes=64)
+            scales = stage.tile([P, units, P], U8, tag="att_scales", align_bytes=64)
+            nc.vector.quantize_mx(
+                out=codes[:].rearrange("p n t -> p (n t)").bitcast(FP8X4),
+                scales=scales[:].rearrange("p n t -> p (n t)"),
+                in_=att_grouped[j][:],
+            )
+            att_q[j] = (codes, scales)
+
+        def head_matmul(j, m):
+            if m == 0:
+                grouped = stage.tile([P, HEADS, P, PACK], BF16, tag="cat_grouped", align_bytes=64)
+                cat_grouped[j] = grouped
+            codes, scales = att_q[j]
+            passes = key_passes(j)
+            cat_ps = psum_cat.tile([P, PACK, P], F32, tag="cat_ps")
+            for a in range(PACK):
+                cols = slice(a * P, (a + 1) * P)
+                for g in range(passes):
+                    nc.tensor.matmul_mx(
+                        out=cat_ps[:, a, :],
+                        lhsT=pz_codes[m][g][:, cols].bitcast(FP8X4),
+                        lhsT_scale=pz_scales[m][g][:, cols],
+                        rhs=codes[:, m * passes + g, :].bitcast(FP8X4),
+                        rhs_scale=scales[:, m * passes + g, :],
+                        start=(g == 0),
+                        stop=(g == passes - 1),
+                    )
+            nc.scalar.copy(out=cat_grouped[j][:, m, :, :], in_=cat_ps[:].rearrange("p a t -> p t a"))
+
+        def quantise_cat(j):
+            codes = stage.tile([P, HEADS, P], U32, tag="cat_codes", align_bytes=64)
+            scales = stage.tile([P, HEADS, P], U8, tag="cat_scales", align_bytes=64)
+            nc.vector.quantize_mx(
+                out=codes[:].rearrange("p m t -> p (m t)").bitcast(FP8X4),
+                scales=scales[:].rearrange("p m t -> p (m t)"),
+                in_=cat_grouped[j][:].rearrange("p m t a -> p (m t a)"),
+            )
+            cat_q[j] = (codes, scales)
+
+        def project(j):
+            codes, scales = cat_q[j]
+            y_bank = psum_y.tile([P, D], F32, tag="y_ps")
+            for m in range(HEADS):
+                nc.tensor.matmul_mx(
+                    out=y_bank[:],
+                    lhsT=codes[:, m, :].bitcast(FP8X4),
+                    lhsT_scale=scales[:, m, :],
+                    rhs=wo_codes[m][:].bitcast(FP8X4),
+                    rhs_scale=wo_scales[m][:],
+                    start=(m == 0),
+                    stop=(m == HEADS - 1),
+                )
+            y_ps[j] = y_bank
+
+        def add_bias_to_x(j):
+            x_plus_bo = stage.tile([P, D], F32, tag="xb")
+            nc.vector.tensor_tensor(out=x_plus_bo[:], in0=x_sb[:, j, :], in1=bo_bc[:], op=ALU.add)
+            xb[j] = x_plus_bo
+
+        def residual(j):
+            h_tile = stage.tile([P, D], F32, tag="h", bufs=3)
+            hsum = stats.tile([P, 1], F32, tag="hsum")
+            nc.vector.scalar_tensor_tensor(
+                out=h_tile[:], in0=y_ps[j][:], scalar=1.0, in1=xb[j][:], op0=ALU.mult, op1=ALU.add,
+                accum_out=hsum[:],
+            )
+            minus_mean = stats.tile([P, 1], F32, tag="negmean")
+            nc.vector.tensor_scalar(
+                out=minus_mean[:], in0=hsum[:], scalar1=-1.0 / D, scalar2=None, op0=ALU.mult
+            )
+            h[j] = h_tile
+            negmean[j] = minus_mean
+
+        def deviation(j):
+            squares = stage.tile([P, D], BF16, tag="squares")
+            ssq = stats.tile([P, 1], F32, tag="ssq")
+            nc.scalar.activation(
+                out=squares[:], in_=h[j][:], func=ACT.Square, bias=negmean[j][:], scale=1.0,
+                accum_out=ssq[:],
+            )
+            root = stats.tile([P, 1], F32, tag="std")
+            nc.scalar.activation(out=root[:], in_=ssq[:], func=ACT.Sqrt, bias=eps_col[:], scale=1.0 / D)
+            std[j] = root
+
+        def centre(j):
+            scaled = stage.tile([P, D], F32, tag="centred")
+            nc.vector.scalar_tensor_tensor(
+                out=scaled[:], in0=h[j][:], scalar=negmean[j][:], in1=gamma_bc[:],
+                op0=ALU.add, op1=ALU.mult,
+            )
+            centred[j] = scaled
+
+        def finish(j):
+            rstd = stats.tile([P, 1], F32, tag="rstd")
+            nc.vector.reciprocal(out=rstd[:], in_=std[j][:])
+            result = stage.tile([P, D], F32, tag="result", bufs=3)
+            nc.vector.scalar_tensor_tensor(
+                out=result[:], in0=centred[j][:], scalar=rstd[:], in1=beta_bc[:],
+                op0=ALU.mult, op1=ALU.add,
+            )
+            nc.sync.dma_start(out=out[0, j * P : (j + 1) * P, :], in_=result[:])
+
+        transpose_attn(0)
+        regroup_pz(0, 0)
+        quantise_pz(0, 0)
+        quantise_attn(0)
+        for m in range(HEADS):
+            if m > 0:
+                regroup_pz(m, 0)
+                quantise_pz(m, 0)
+                quantise_wo(m - 1)
+            transpose_wo(m)
+            head_matmul(0, m)
+        quantise_wo(HEADS - 1)
+        transpose_attn(1)
+        quantise_attn(1)
+        transpose_attn(2)
+        regroup_pz(0, 1)
+        quantise_pz(0, 1)
+
+        for r in range(1, TILES + 2):
+            if r < TILES:
+                for m in range(HEADS):
+                    head_matmul(r, m)
+            if r < HEADS:
+                regroup_pz(r, 1)
+            if r - 1 < TILES:
+                quantise_cat(r - 1)
+                project(r - 1)
+                add_bias_to_x(r - 1)
+            if r >= 2:
+                deviation(r - 2)
+            if r + 2 < TILES:
+                transpose_attn(r + 2)
+            if r + 1 < TILES:
+                quantise_attn(r + 1)
+            if r < HEADS:
+                quantise_pz(r, 1)
+            if r >= 2:
+                centre(r - 2)
+            if r - 1 < TILES:
+                residual(r - 1)
+            if r >= 2:
+                finish(r - 2)

@@ -100,8 +100,6 @@ def tile_softmaxattention_pb_kernel(tc, attn, pz, Wo, bo, x, gamma, beta, out):
 
         ident_f32 = const.tile([P, P], F32)
         make_identity(nc, ident_f32[:])
-        ident_bf16 = const.tile([P, P], BF16)
-        make_identity(nc, ident_bf16[:])
         ones = const.tile([P, P], BF16)
         nc.vector.memset(ones[:], 1.0)
         eps_col = const.tile([P, 1], F32)
@@ -138,36 +136,34 @@ def tile_softmaxattention_pb_kernel(tc, attn, pz, Wo, bo, x, gamma, beta, out):
         wo_grouped = {}
 
         def regroup_pz(m, g):
-            grouped = stage.tile([P, D, PACK], BF16, tag="w_grouped", bufs=3, align_bytes=64)
-            nc.vector.tensor_copy(
-                out=grouped[:].rearrange("p (c i) k -> p c k i", i=4),
-                in_=pz_raw[m][g][:].rearrange("p k (c i) -> p c k i", i=4),
-            )
+            grouped = stage.tile([P, D * PACK], BF16, tag="w_grouped", bufs=3, align_bytes=64)
+            dst = grouped[:].rearrange("p (u e c i k) -> p u c k e i", u=2, e=2, i=4, k=PACK)
+            src = pz_raw[m][g][:].rearrange("p k (u c i e) -> p u c k e i", u=2, e=2, i=4)
+            for u in range(2):
+                nc.vector.tensor_copy(out=dst[:, u], in_=src[:, u])
             pz_grouped[(m, g)] = grouped
 
         def quantise_pz(m, g):
             nc.vector.quantize_mx(
                 out=pz_codes[m][g][:].bitcast(FP8X4),
                 scales=pz_scales[m][g][:],
-                in_=pz_grouped[(m, g)][:].rearrange("p i k -> p (i k)"),
+                in_=pz_grouped[(m, g)][:],
             )
 
         def transpose_wo(m):
-            grouped = stage.tile([P, D, PACK], BF16, tag="w_grouped", bufs=3, align_bytes=64)
+            grouped = stage.tile([P, D * PACK], BF16, tag="w_grouped", bufs=3, align_bytes=64)
+            words = grouped[:].bitcast(F32).rearrange("p (r q u) -> p r q u", q=P, u=2)
             for half in range(2):
-                wo_t = psum_t.tile([P, 2, PACK, P], BF16, tag="tp")
+                wo_t = psum_t.tile([P, 2, 2, P], F32, tag="tp")
                 for r in range(2):
-                    for a in range(PACK):
+                    for u in range(2):
                         nc.tensor.transpose(
-                            wo_t[:, r, a, :],
-                            wo_raw[m][:, 2 * half + r, a * P : (a + 1) * P],
-                            ident_bf16[:],
+                            wo_t[:, r, u, :],
+                            wo_raw[m][:, 2 * half + r, u * HALF_PASS : (u + 1) * HALF_PASS].bitcast(F32),
+                            ident_f32[:],
                         )
                 nc.scalar.copy(
-                    out=grouped[:, 2 * half * P : 2 * (half + 1) * P, :].rearrange(
-                        "p (r q) a -> p r q a", r=2
-                    ),
-                    in_=wo_t[:].rearrange("p r a q -> p r q a"),
+                    out=words[:, 2 * half : 2 * half + 2, :, :], in_=wo_t[:].rearrange("p r u q -> p r q u")
                 )
             wo_grouped[m] = grouped
 
@@ -175,7 +171,7 @@ def tile_softmaxattention_pb_kernel(tc, attn, pz, Wo, bo, x, gamma, beta, out):
             nc.vector.quantize_mx(
                 out=wo_codes[m][:].bitcast(FP8X4),
                 scales=wo_scales[m][:],
-                in_=wo_grouped[m][:].rearrange("p o a -> p (o a)"),
+                in_=wo_grouped[m][:],
             )
 
         att_grouped = {}
@@ -212,8 +208,8 @@ def tile_softmaxattention_pb_kernel(tc, attn, pz, Wo, bo, x, gamma, beta, out):
 
         def quantise_attn(j):
             units = HEADS * key_passes(j)
-            codes = stage.tile([P, units, P], U32, tag="att_codes", align_bytes=64)
-            scales = stage.tile([P, units, P], U8, tag="att_scales", align_bytes=64)
+            codes = stage.tile([P, units, P], U32, tag="att_codes", bufs=4, align_bytes=64)
+            scales = stage.tile([P, units, P], U8, tag="att_scales", bufs=4, align_bytes=64)
             nc.vector.quantize_mx(
                 out=codes[:].rearrange("p n t -> p (n t)").bitcast(FP8X4),
                 scales=scales[:].rearrange("p n t -> p (n t)"),
@@ -332,6 +328,8 @@ def tile_softmaxattention_pb_kernel(tc, attn, pz, Wo, bo, x, gamma, beta, out):
         transpose_attn(2)
         regroup_pz(0, 1)
         quantise_pz(0, 1)
+        quantise_attn(2)
+        transpose_attn(3)
 
         for r in range(1, TILES + 2):
             if r < TILES:
@@ -345,10 +343,10 @@ def tile_softmaxattention_pb_kernel(tc, attn, pz, Wo, bo, x, gamma, beta, out):
                 add_bias_to_x(r - 1)
             if r >= 2:
                 deviation(r - 2)
+            if r + 3 < TILES:
+                transpose_attn(r + 3)
             if r + 2 < TILES:
-                transpose_attn(r + 2)
-            if r + 1 < TILES:
-                quantise_attn(r + 1)
+                quantise_attn(r + 2)
             if r < HEADS:
                 quantise_pz(r, 1)
             if r >= 2:

@@ -30,6 +30,10 @@ def key_passes(j):
     return (j * P) // CAUSAL_BLOCK + 1
 
 
+def seen_keys(j):
+    return (j + 1) * P
+
+
 def tile_softmaxattention_pb_kernel(tc, attn, pz, Wo, bo, x, gamma, beta, out):
     nc = tc.nc
     with ExitStack() as ctx:
@@ -68,9 +72,11 @@ def tile_softmaxattention_pb_kernel(tc, attn, pz, Wo, bo, x, gamma, beta, out):
             )
 
         def load_attn(j):
-            keys = key_passes(j) * K_PASS
+            keys = seen_keys(j)
+            if keys < key_passes(j) * K_PASS:
+                nc.gpsimd.memset(attn_raw[j][:, :, keys:].bitcast(F32), 0.0)
             nc.sync.dma_start(
-                out=attn_raw[j][:],
+                out=attn_raw[j][:, :, 0:keys],
                 in_=attn[0, :, j * P : (j + 1) * P, 0:keys].rearrange("m p s -> p m s"),
             )
 
@@ -83,10 +89,10 @@ def tile_softmaxattention_pb_kernel(tc, attn, pz, Wo, bo, x, gamma, beta, out):
 
         load_pz(0, 0)
         load_attn(0)
-        load_wo(0)
         for m in range(1, HEADS):
             load_pz(m, 0)
-            load_wo(m)
+            load_wo(m - 1)
+        load_wo(HEADS - 1)
         load_attn(1)
         load_attn(2)
         load_pz(0, 1)
@@ -113,7 +119,7 @@ def tile_softmaxattention_pb_kernel(tc, attn, pz, Wo, bo, x, gamma, beta, out):
         nc.vector.tensor_copy(out=vec_rows[0:1, :, :], in_=vec_loaded[:])
         spread = []
         warm = const.tile([P, 1], F32)
-        nc.scalar.activation(out=warm[:], in_=eps_col[:], func=ACT.Sqrt)
+        nc.scalar.activation(out=warm[:], in_=eps_col[:], func=ACT.Abs_reciprocal_sqrt)
         for k in range(3):
             vec_ps = psum_t.tile([P, D], F32, tag="tp")
             nc.tensor.matmul(out=vec_ps[:], lhsT=ones[:], rhs=vec_rows[:, k, :], start=True, stop=True)
@@ -181,8 +187,9 @@ def tile_softmaxattention_pb_kernel(tc, attn, pz, Wo, bo, x, gamma, beta, out):
         y_ps = {}
         xb = {}
         h = {}
+        hsum = {}
         negmean = {}
-        std = {}
+        rstd = {}
         centred = {}
 
         def transpose_attn(j):
@@ -270,16 +277,19 @@ def tile_softmaxattention_pb_kernel(tc, attn, pz, Wo, bo, x, gamma, beta, out):
 
         def residual(j):
             h_tile = stage.tile([P, D], F32, tag="h", bufs=3)
-            hsum = stats.tile([P, 1], F32, tag="hsum")
+            row_sum = stats.tile([P, 1], F32, tag="hsum")
             nc.vector.scalar_tensor_tensor(
                 out=h_tile[:], in0=y_ps[j][:], scalar=1.0, in1=xb[j][:], op0=ALU.mult, op1=ALU.add,
-                accum_out=hsum[:],
-            )
-            minus_mean = stats.tile([P, 1], F32, tag="negmean")
-            nc.vector.tensor_scalar(
-                out=minus_mean[:], in0=hsum[:], scalar1=-1.0 / D, scalar2=None, op0=ALU.mult
+                accum_out=row_sum[:],
             )
             h[j] = h_tile
+            hsum[j] = row_sum
+
+        def negate_mean(j):
+            minus_mean = stats.tile([P, 1], F32, tag="negmean")
+            nc.vector.tensor_scalar(
+                out=minus_mean[:], in0=hsum[j][:], scalar1=-1.0 / D, scalar2=None, op0=ALU.mult
+            )
             negmean[j] = minus_mean
 
         def deviation(j):
@@ -289,9 +299,11 @@ def tile_softmaxattention_pb_kernel(tc, attn, pz, Wo, bo, x, gamma, beta, out):
                 out=squares[:], in_=h[j][:], func=ACT.Square, bias=negmean[j][:], scale=1.0,
                 accum_out=ssq[:],
             )
-            root = stats.tile([P, 1], F32, tag="std")
-            nc.scalar.activation(out=root[:], in_=ssq[:], func=ACT.Sqrt, bias=eps_col[:], scale=1.0 / D)
-            std[j] = root
+            inv_std = stats.tile([P, 1], F32, tag="rstd")
+            nc.scalar.activation(
+                out=inv_std[:], in_=ssq[:], func=ACT.Abs_reciprocal_sqrt, bias=eps_col[:], scale=1.0 / D
+            )
+            rstd[j] = inv_std
 
         def centre(j):
             scaled = stage.tile([P, D], F32, tag="centred")
@@ -302,11 +314,9 @@ def tile_softmaxattention_pb_kernel(tc, attn, pz, Wo, bo, x, gamma, beta, out):
             centred[j] = scaled
 
         def finish(j):
-            rstd = stats.tile([P, 1], F32, tag="rstd")
-            nc.vector.reciprocal(out=rstd[:], in_=std[j][:])
             result = stage.tile([P, D], F32, tag="result", bufs=3)
             nc.vector.scalar_tensor_tensor(
-                out=result[:], in0=centred[j][:], scalar=rstd[:], in1=beta_bc[:],
+                out=result[:], in0=centred[j][:], scalar=rstd[j][:], in1=beta_bc[:],
                 op0=ALU.mult, op1=ALU.add,
             )
             nc.sync.dma_start(out=out[0, j * P : (j + 1) * P, :], in_=result[:])
@@ -355,3 +365,5 @@ def tile_softmaxattention_pb_kernel(tc, attn, pz, Wo, bo, x, gamma, beta, out):
                 residual(r - 1)
             if r >= 2:
                 finish(r - 2)
+            if r - 1 < TILES:
+                negate_mean(r - 1)

@@ -42,9 +42,12 @@ def tile_softmaxattention_pb_kernel(tc, attn, pz, Wo, bo, x, gamma, beta, out):
         weights = ctx.enter_context(tc.tile_pool(name="weights", bufs=1))
         stage = ctx.enter_context(tc.tile_pool(name="stage", bufs=2))
         stats = ctx.enter_context(tc.tile_pool(name="stats", bufs=3))
-        psum_t = ctx.enter_context(tc.psum_pool(name="psum_t", bufs=3))
-        psum_cat = ctx.enter_context(tc.psum_pool(name="psum_cat", bufs=HEADS))
+        psum_t = ctx.enter_context(tc.psum_pool(name="psum_t", bufs=4))
+        psum_cat = ctx.enter_context(tc.psum_pool(name="psum_cat", bufs=3))
         psum_y = ctx.enter_context(tc.psum_pool(name="psum_y", bufs=1))
+
+        vec_rows = const.tile([P, 3, D], BF16)
+        nc.gpsimd.memset(vec_rows[:].bitcast(F32), 0.0)
 
         pz_raw = [
             [inputs.tile([P, PACK, D], BF16, name="pz_raw_%d_%d" % (m, g)) for g in range(2)]
@@ -89,20 +92,26 @@ def tile_softmaxattention_pb_kernel(tc, attn, pz, Wo, bo, x, gamma, beta, out):
 
         load_pz(0, 0)
         load_attn(0)
-        for m in range(1, HEADS):
-            load_pz(m, 0)
-            load_wo(m - 1)
-        load_wo(HEADS - 1)
+        load_pz(1, 0)
         load_attn(1)
-        load_attn(2)
-        load_pz(0, 1)
+        load_pz(2, 0)
+        load_wo(0)
+        load_pz(3, 0)
+        load_wo(1)
         load_x(0)
-        for m in range(1, HEADS):
-            load_attn(2 + m)
-            load_pz(m, 1)
+        load_attn(2)
+        load_wo(2)
+        load_wo(3)
+        load_pz(0, 1)
+        load_attn(3)
+        load_pz(1, 1)
+        load_attn(4)
+        load_pz(2, 1)
+        load_attn(5)
+        load_pz(3, 1)
+        load_x(1)
         load_attn(6)
         load_attn(7)
-        load_x(1)
 
         ident_f32 = const.tile([P, P], F32)
         make_identity(nc, ident_f32[:])
@@ -111,22 +120,18 @@ def tile_softmaxattention_pb_kernel(tc, attn, pz, Wo, bo, x, gamma, beta, out):
         eps_col = const.tile([P, 1], F32)
         nc.vector.memset(eps_col[:], LN_EPS)
 
-        vec_loaded = const.tile([1, 3, D], BF16)
         for k, vec in enumerate((bo, gamma, beta)):
-            nc.scalar.dma_start(out=vec_loaded[0:1, k, :], in_=vec.rearrange("(o n) -> o n", o=1))
-        vec_rows = const.tile([P, 3, D], BF16)
-        nc.vector.memset(vec_rows[:], 0.0)
-        nc.vector.tensor_copy(out=vec_rows[0:1, :, :], in_=vec_loaded[:])
-        spread = []
+            nc.scalar.dma_start(out=vec_rows[0:1, k, :], in_=vec.rearrange("(o n) -> o n", o=1))
         warm = const.tile([P, 1], F32)
         nc.scalar.activation(out=warm[:], in_=eps_col[:], func=ACT.Abs_reciprocal_sqrt)
-        for k in range(3):
-            vec_ps = psum_t.tile([P, D], F32, tag="tp")
-            nc.tensor.matmul(out=vec_ps[:], lhsT=ones[:], rhs=vec_rows[:, k, :], start=True, stop=True)
-            vec_bc = const.tile([P, D], F32, name="vec_bc_%d" % k)
-            nc.scalar.copy(out=vec_bc[:], in_=vec_ps[:])
-            spread.append(vec_bc)
-        bo_bc, gamma_bc, beta_bc = spread
+        vec_bc = [const.tile([P, D], F32, name="vec_bc_%d" % k) for k in range(3)]
+        bo_bc, gamma_bc, beta_bc = vec_bc
+
+        def spread_vectors():
+            for k in range(3):
+                vec_ps = psum_t.tile([P, D], F32, tag="tp")
+                nc.tensor.matmul(out=vec_ps[:], lhsT=ones[:], rhs=vec_rows[:, k, :], start=True, stop=True)
+                nc.scalar.copy(out=vec_bc[k][:], in_=vec_ps[:])
 
         pz_codes = [
             [weights.tile([P, D], U32, name="pz_codes_%d_%d" % (m, g), align_bytes=64) for g in range(2)]
@@ -141,13 +146,13 @@ def tile_softmaxattention_pb_kernel(tc, attn, pz, Wo, bo, x, gamma, beta, out):
         pz_grouped = {}
         wo_grouped = {}
 
-        def regroup_pz(m, g):
-            grouped = stage.tile([P, D * PACK], BF16, tag="w_grouped", bufs=3, align_bytes=64)
-            dst = grouped[:].rearrange("p (u e c i k) -> p u c k e i", u=2, e=2, i=4, k=PACK)
+        def regroup_pz(m, g, u):
+            if u == 0:
+                grouped = stage.tile([P, D * PACK], BF16, tag="pz_grouped", align_bytes=64)
+                pz_grouped[(m, g)] = grouped
+            dst = pz_grouped[(m, g)][:].rearrange("p (u e c i k) -> p u c k e i", u=2, e=2, i=4, k=PACK)
             src = pz_raw[m][g][:].rearrange("p k (u c i e) -> p u c k e i", u=2, e=2, i=4)
-            for u in range(2):
-                nc.vector.tensor_copy(out=dst[:, u], in_=src[:, u])
-            pz_grouped[(m, g)] = grouped
+            nc.vector.tensor_copy(out=dst[:, u], in_=src[:, u])
 
         def quantise_pz(m, g):
             nc.vector.quantize_mx(
@@ -157,7 +162,7 @@ def tile_softmaxattention_pb_kernel(tc, attn, pz, Wo, bo, x, gamma, beta, out):
             )
 
         def transpose_wo(m):
-            grouped = stage.tile([P, D * PACK], BF16, tag="w_grouped", bufs=3, align_bytes=64)
+            grouped = stage.tile([P, D * PACK], BF16, tag="wo_grouped", align_bytes=64)
             words = grouped[:].bitcast(F32).rearrange("p (r q u) -> p r q u", q=P, u=2)
             for half in range(2):
                 wo_t = psum_t.tile([P, 2, 2, P], F32, tag="tp")
@@ -189,6 +194,7 @@ def tile_softmaxattention_pb_kernel(tc, attn, pz, Wo, bo, x, gamma, beta, out):
         h = {}
         hsum = {}
         negmean = {}
+        ssqs = {}
         rstd = {}
         centred = {}
 
@@ -271,12 +277,12 @@ def tile_softmaxattention_pb_kernel(tc, attn, pz, Wo, bo, x, gamma, beta, out):
             y_ps[j] = y_bank
 
         def add_bias_to_x(j):
-            x_plus_bo = stage.tile([P, D], F32, tag="xb")
+            x_plus_bo = stage.tile([P, D], F32, tag="xb", bufs=4)
             nc.vector.tensor_tensor(out=x_plus_bo[:], in0=x_sb[:, j, :], in1=bo_bc[:], op=ALU.add)
             xb[j] = x_plus_bo
 
         def residual(j):
-            h_tile = stage.tile([P, D], F32, tag="h", bufs=3)
+            h_tile = stage.tile([P, D], F32, tag="h")
             row_sum = stats.tile([P, 1], F32, tag="hsum")
             nc.vector.scalar_tensor_tensor(
                 out=h_tile[:], in0=y_ps[j][:], scalar=1.0, in1=xb[j][:], op0=ALU.mult, op1=ALU.add,
@@ -299,9 +305,12 @@ def tile_softmaxattention_pb_kernel(tc, attn, pz, Wo, bo, x, gamma, beta, out):
                 out=squares[:], in_=h[j][:], func=ACT.Square, bias=negmean[j][:], scale=1.0,
                 accum_out=ssq[:],
             )
+            ssqs[j] = ssq
+
+        def inverse_std(j):
             inv_std = stats.tile([P, 1], F32, tag="rstd")
             nc.scalar.activation(
-                out=inv_std[:], in_=ssq[:], func=ACT.Abs_reciprocal_sqrt, bias=eps_col[:], scale=1.0 / D
+                out=inv_std[:], in_=ssqs[j][:], func=ACT.Abs_reciprocal_sqrt, bias=eps_col[:], scale=1.0 / D
             )
             rstd[j] = inv_std
 
@@ -314,56 +323,100 @@ def tile_softmaxattention_pb_kernel(tc, attn, pz, Wo, bo, x, gamma, beta, out):
             centred[j] = scaled
 
         def finish(j):
-            result = stage.tile([P, D], F32, tag="result", bufs=3)
+            result = stage.tile([P, D], F32, tag="result")
             nc.vector.scalar_tensor_tensor(
                 out=result[:], in0=centred[j][:], scalar=rstd[j][:], in1=beta_bc[:],
                 op0=ALU.mult, op1=ALU.add,
             )
             nc.sync.dma_start(out=out[0, j * P : (j + 1) * P, :], in_=result[:])
 
+        ctx.enter_context(tc.manual_schedule())
         transpose_attn(0)
-        regroup_pz(0, 0)
+        spread_vectors()
+        transpose_attn(1)
+        regroup_pz(0, 0, 0)
+        regroup_pz(0, 0, 1)
+        regroup_pz(1, 0, 0)
         quantise_pz(0, 0)
         quantise_attn(0)
-        for m in range(HEADS):
-            if m > 0:
-                regroup_pz(m, 0)
-                quantise_pz(m, 0)
-                quantise_wo(m - 1)
-            transpose_wo(m)
-            head_matmul(0, m)
-        quantise_wo(HEADS - 1)
-        transpose_attn(1)
+        regroup_pz(1, 0, 1)
+        head_matmul(0, 0)
+        regroup_pz(2, 0, 0)
+        quantise_pz(1, 0)
         quantise_attn(1)
+        regroup_pz(2, 0, 1)
+        transpose_wo(0)
+        head_matmul(1, 0)
+        head_matmul(0, 1)
+        head_matmul(1, 1)
+        regroup_pz(3, 0, 0)
+        quantise_pz(2, 0)
+        quantise_wo(0)
+        regroup_pz(3, 0, 1)
+        transpose_wo(1)
+        head_matmul(0, 2)
+        head_matmul(1, 2)
+        add_bias_to_x(0)
+        quantise_pz(3, 0)
+        add_bias_to_x(1)
+        quantise_wo(1)
         transpose_attn(2)
-        regroup_pz(0, 1)
-        quantise_pz(0, 1)
+        head_matmul(0, 3)
+        head_matmul(1, 3)
+        transpose_wo(2)
+        transpose_wo(3)
+        quantise_cat(0)
         quantise_attn(2)
-        transpose_attn(3)
+        quantise_cat(1)
+        quantise_wo(2)
+        regroup_pz(0, 1, 0)
+        regroup_pz(0, 1, 1)
+        quantise_wo(3)
+        add_bias_to_x(2)
+        quantise_pz(0, 1)
 
-        for r in range(1, TILES + 2):
-            if r < TILES:
-                for m in range(HEADS):
+        for r in range(2, TILES + 2):
+            for m in range(HEADS):
+                if m == 1 and r >= 3:
+                    deviation(r - 3)
+                if m == 2:
+                    project(r - 2)
+                if r < TILES:
                     head_matmul(r, m)
-            if r < HEADS:
-                regroup_pz(r, 1)
-            if r - 1 < TILES:
-                quantise_cat(r - 1)
-                project(r - 1)
-                add_bias_to_x(r - 1)
-            if r >= 2:
-                deviation(r - 2)
-            if r + 3 < TILES:
-                transpose_attn(r + 3)
+                if m == 1 and r >= 3:
+                    inverse_std(r - 3)
+            if r == 2:
+                transpose_attn(3)
             if r + 2 < TILES:
-                quantise_attn(r + 2)
-            if r < HEADS:
-                quantise_pz(r, 1)
-            if r >= 2:
+                transpose_attn(r + 2)
+            if r == 2:
+                regroup_pz(1, 1, 0)
+                regroup_pz(1, 1, 1)
+            if r == 3:
+                regroup_pz(3, 1, 0)
+                regroup_pz(3, 1, 1)
+            if r + 1 < TILES:
+                add_bias_to_x(r + 1)
+            if r == 2:
+                regroup_pz(2, 1, 0)
+                quantise_pz(1, 1)
+                regroup_pz(2, 1, 1)
+            if r == 3:
+                quantise_pz(3, 1)
+            if r == 2:
+                quantise_attn(3)
+                quantise_pz(2, 1)
+            elif r + 1 < TILES:
+                quantise_attn(r + 1)
+            if 2 < r <= TILES:
+                quantise_cat(r - 1)
+            residual(r - 2)
+            if r >= 3:
+                finish(r - 3)
+            negate_mean(r - 2)
+            if r < TILES + 1:
                 centre(r - 2)
-            if r - 1 < TILES:
-                residual(r - 1)
-            if r >= 2:
-                finish(r - 2)
-            if r - 1 < TILES:
-                negate_mean(r - 1)
+        deviation(TILES - 1)
+        inverse_std(TILES - 1)
+        centre(TILES - 1)
+        finish(TILES - 1)

@@ -46,9 +46,6 @@ def tile_softmaxattention_pb_kernel(tc, attn, pz, Wo, bo, x, gamma, beta, out):
         psum_cat = ctx.enter_context(tc.psum_pool(name="psum_cat", bufs=3))
         psum_y = ctx.enter_context(tc.psum_pool(name="psum_y", bufs=1))
 
-        vec_rows = const.tile([P, 3, D], BF16)
-        nc.gpsimd.memset(vec_rows[:].bitcast(F32), 0.0)
-
         pz_raw = [
             [inputs.tile([P, PACK, D], BF16, name="pz_raw_%d_%d" % (m, g)) for g in range(2)]
             for m in range(HEADS)
@@ -92,6 +89,8 @@ def tile_softmaxattention_pb_kernel(tc, attn, pz, Wo, bo, x, gamma, beta, out):
 
         load_pz(0, 0)
         load_attn(0)
+        vec_rows = const.tile([P, 3, D], BF16)
+        nc.gpsimd.memset(vec_rows[:].bitcast(F32), 0.0)
         load_pz(1, 0)
         load_attn(1)
         load_pz(2, 0)
@@ -146,13 +145,13 @@ def tile_softmaxattention_pb_kernel(tc, attn, pz, Wo, bo, x, gamma, beta, out):
         pz_grouped = {}
         wo_grouped = {}
 
-        def regroup_pz(m, g, u):
-            if u == 0:
-                grouped = stage.tile([P, D * PACK], BF16, tag="pz_grouped", align_bytes=64)
-                pz_grouped[(m, g)] = grouped
-            dst = pz_grouped[(m, g)][:].rearrange("p (u e c i k) -> p u c k e i", u=2, e=2, i=4, k=PACK)
-            src = pz_raw[m][g][:].rearrange("p k (u c i e) -> p u c k e i", u=2, e=2, i=4)
-            nc.vector.tensor_copy(out=dst[:, u], in_=src[:, u])
+        def regroup_pz(m, g):
+            grouped = stage.tile([P, D * PACK], BF16, tag="pz_grouped", align_bytes=64)
+            nc.vector.tensor_copy(
+                out=grouped[:].rearrange("p (e c i k) -> p c k e i", e=2, i=4, k=PACK),
+                in_=pz_raw[m][g][:].rearrange("p k (c i e) -> p c k e i", i=4, e=2),
+            )
+            pz_grouped[(m, g)] = grouped
 
         def quantise_pz(m, g):
             nc.vector.quantize_mx(
@@ -238,7 +237,8 @@ def tile_softmaxattention_pb_kernel(tc, attn, pz, Wo, bo, x, gamma, beta, out):
             passes = key_passes(j)
             cat_ps = psum_cat.tile([P, PACK, P], F32, tag="cat_ps")
             for a in range(PACK):
-                cols = slice(a * P, (a + 1) * P)
+                u, e = divmod(a, 2)
+                cols = slice((2 * e + u) * P, (2 * e + u + 1) * P)
                 for g in range(passes):
                     nc.tensor.matmul_mx(
                         out=cat_ps[:, a, :],
@@ -293,7 +293,7 @@ def tile_softmaxattention_pb_kernel(tc, attn, pz, Wo, bo, x, gamma, beta, out):
 
         def negate_mean(j):
             minus_mean = stats.tile([P, 1], F32, tag="negmean")
-            nc.vector.tensor_scalar(
+            nc.gpsimd.tensor_scalar(
                 out=minus_mean[:], in0=hsum[j][:], scalar1=-1.0 / D, scalar2=None, op0=ALU.mult
             )
             negmean[j] = minus_mean
@@ -334,32 +334,30 @@ def tile_softmaxattention_pb_kernel(tc, attn, pz, Wo, bo, x, gamma, beta, out):
         transpose_attn(0)
         spread_vectors()
         transpose_attn(1)
-        regroup_pz(0, 0, 0)
-        regroup_pz(0, 0, 1)
-        regroup_pz(1, 0, 0)
+        regroup_pz(0, 0)
         quantise_pz(0, 0)
+        regroup_pz(1, 0)
         quantise_attn(0)
-        regroup_pz(1, 0, 1)
-        head_matmul(0, 0)
-        regroup_pz(2, 0, 0)
         quantise_pz(1, 0)
-        quantise_attn(1)
-        regroup_pz(2, 0, 1)
+        head_matmul(0, 0)
         transpose_wo(0)
+        regroup_pz(2, 0)
+        quantise_attn(1)
+        quantise_pz(2, 0)
         head_matmul(1, 0)
         head_matmul(0, 1)
         head_matmul(1, 1)
-        regroup_pz(3, 0, 0)
-        quantise_pz(2, 0)
+        regroup_pz(3, 0)
         quantise_wo(0)
-        regroup_pz(3, 0, 1)
+        quantise_pz(3, 0)
         transpose_wo(1)
         head_matmul(0, 2)
         head_matmul(1, 2)
         add_bias_to_x(0)
-        quantise_pz(3, 0)
         add_bias_to_x(1)
         quantise_wo(1)
+        add_bias_to_x(2)
+        add_bias_to_x(3)
         transpose_attn(2)
         head_matmul(0, 3)
         head_matmul(1, 3)
@@ -369,13 +367,18 @@ def tile_softmaxattention_pb_kernel(tc, attn, pz, Wo, bo, x, gamma, beta, out):
         quantise_attn(2)
         quantise_cat(1)
         quantise_wo(2)
-        regroup_pz(0, 1, 0)
-        regroup_pz(0, 1, 1)
+        regroup_pz(0, 1)
         quantise_wo(3)
-        add_bias_to_x(2)
         quantise_pz(0, 1)
+        transpose_attn(3)
 
         for r in range(2, TILES + 2):
+            if r <= HEADS:
+                regroup_pz(r - 1, 1)
+            if 4 <= r + 1 < TILES:
+                add_bias_to_x(r + 1)
+            if r <= HEADS:
+                quantise_pz(r - 1, 1)
             for m in range(HEADS):
                 if m == 1 and r >= 3:
                     deviation(r - 3)
@@ -385,35 +388,18 @@ def tile_softmaxattention_pb_kernel(tc, attn, pz, Wo, bo, x, gamma, beta, out):
                     head_matmul(r, m)
                 if m == 1 and r >= 3:
                     inverse_std(r - 3)
-            if r == 2:
-                transpose_attn(3)
-            if r + 2 < TILES:
+            if 4 <= r + 2 < TILES:
                 transpose_attn(r + 2)
-            if r == 2:
-                regroup_pz(1, 1, 0)
-                regroup_pz(1, 1, 1)
-            if r == 3:
-                regroup_pz(3, 1, 0)
-                regroup_pz(3, 1, 1)
             if r + 1 < TILES:
-                add_bias_to_x(r + 1)
-            if r == 2:
-                regroup_pz(2, 1, 0)
-                quantise_pz(1, 1)
-                regroup_pz(2, 1, 1)
-            if r == 3:
-                quantise_pz(3, 1)
-            if r == 2:
-                quantise_attn(3)
-                quantise_pz(2, 1)
-            elif r + 1 < TILES:
                 quantise_attn(r + 1)
-            if 2 < r <= TILES:
+            if 6 <= r <= TILES:
                 quantise_cat(r - 1)
             residual(r - 2)
+            negate_mean(r - 2)
             if r >= 3:
                 finish(r - 3)
-            negate_mean(r - 2)
+            if 2 < r < 6:
+                quantise_cat(r - 1)
             if r < TILES + 1:
                 centre(r - 2)
         deviation(TILES - 1)

@@ -19,6 +19,7 @@ HEADS = 4
 T = 1024
 D = 512
 TILES = T // P
+VEC_ROWS = D // P
 CAUSAL_BLOCK = 512
 LN_EPS = 1e-5
 
@@ -28,6 +29,10 @@ BYTES = 2 * (HEADS * T * (T + 1) // 2 + HEADS * T * D + D * HEADS * D + T * D + 
 
 def key_passes(j):
     return (j * P) // CAUSAL_BLOCK + 1
+
+
+def half_passes(j):
+    return -(-seen_keys(j) // HALF_PASS)
 
 
 def seen_keys(j):
@@ -46,13 +51,52 @@ def tile_softmaxattention_pb_kernel(tc, attn, pz, Wo, bo, x, gamma, beta, out):
         psum_cat = ctx.enter_context(tc.psum_pool(name="psum_cat", bufs=3))
         psum_y = ctx.enter_context(tc.psum_pool(name="psum_y", bufs=1))
 
+        ctx.enter_context(tc.manual_schedule())
+
+        ident_f32 = const.tile([P, P], F32)
+        make_identity(nc, ident_f32[:])
+        zero_words = const.tile([P, P], F32)
+        nc.gpsimd.memset(zero_words[:], 0.0)
+
+        vec_rows = const.tile([P, P], BF16)
+        nc.vector.memset(vec_rows[:].bitcast(F32), 0.0)
+        for k, vec in enumerate((bo, gamma, beta)):
+            nc.scalar.dma_start(
+                out=vec_rows[k * VEC_ROWS : (k + 1) * VEC_ROWS, :], in_=vec.rearrange("(r n) -> r n", n=P)
+            )
+        eps_col = const.tile([P, 1], F32)
+        nc.vector.memset(eps_col[:], LN_EPS)
+        ident_bf16 = const.tile([P, P], BF16)
+        nc.vector.tensor_copy(out=ident_bf16[:], in_=ident_f32[:])
+        warm = const.tile([P, 1], F32)
+        nc.scalar.activation(out=warm[:], in_=eps_col[:], func=ACT.Abs_reciprocal_sqrt)
+        vec_bc = [const.tile([P, D], F32, name="vec_bc_%d" % k) for k in range(3)]
+        bo_bc, gamma_bc, beta_bc = vec_bc
+
+        def spread_row(out_ps, k, r):
+            row = k * VEC_ROWS + r
+            nc.tensor.matmul(
+                out=out_ps[:, r * P : (r + 1) * P],
+                lhsT=ident_bf16[:, row : row + 1].to_broadcast([P, P]),
+                rhs=vec_rows[:],
+                start=True,
+                stop=True,
+            )
+
+        def spread_vectors():
+            for k in range(3):
+                vec_ps = psum_t.tile([P, D], F32, tag="tp")
+                for r in range(VEC_ROWS):
+                    spread_row(vec_ps, k, r)
+                nc.scalar.copy(out=vec_bc[k][:], in_=vec_ps[:])
+
         pz_raw = [
             [inputs.tile([P, PACK, D], BF16, name="pz_raw_%d_%d" % (m, g)) for g in range(2)]
             for m in range(HEADS)
         ]
         wo_raw = [inputs.tile([P, PACK, K_PASS], BF16, name="wo_raw_%d" % m) for m in range(HEADS)]
         attn_raw = [
-            inputs.tile([P, HEADS, key_passes(j) * K_PASS], BF16, name="attn_raw_%d" % j)
+            inputs.tile([P, HEADS, half_passes(j) * HALF_PASS], BF16, name="attn_raw_%d" % j)
             for j in range(TILES)
         ]
         x_sb = inputs.tile([P, TILES, D], BF16)
@@ -73,7 +117,7 @@ def tile_softmaxattention_pb_kernel(tc, attn, pz, Wo, bo, x, gamma, beta, out):
 
         def load_attn(j):
             keys = seen_keys(j)
-            if keys < key_passes(j) * K_PASS:
+            if keys < half_passes(j) * HALF_PASS:
                 nc.gpsimd.memset(attn_raw[j][:, :, keys:].bitcast(F32), 0.0)
             nc.sync.dma_start(
                 out=attn_raw[j][:, :, 0:keys],
@@ -89,8 +133,6 @@ def tile_softmaxattention_pb_kernel(tc, attn, pz, Wo, bo, x, gamma, beta, out):
 
         load_pz(0, 0)
         load_attn(0)
-        vec_rows = const.tile([P, 3, D], BF16)
-        nc.gpsimd.memset(vec_rows[:].bitcast(F32), 0.0)
         load_pz(1, 0)
         load_attn(1)
         load_pz(2, 0)
@@ -111,26 +153,6 @@ def tile_softmaxattention_pb_kernel(tc, attn, pz, Wo, bo, x, gamma, beta, out):
         load_x(1)
         load_attn(6)
         load_attn(7)
-
-        ident_f32 = const.tile([P, P], F32)
-        make_identity(nc, ident_f32[:])
-        ones = const.tile([P, P], BF16)
-        nc.vector.memset(ones[:], 1.0)
-        eps_col = const.tile([P, 1], F32)
-        nc.vector.memset(eps_col[:], LN_EPS)
-
-        for k, vec in enumerate((bo, gamma, beta)):
-            nc.scalar.dma_start(out=vec_rows[0:1, k, :], in_=vec.rearrange("(o n) -> o n", o=1))
-        warm = const.tile([P, 1], F32)
-        nc.scalar.activation(out=warm[:], in_=eps_col[:], func=ACT.Abs_reciprocal_sqrt)
-        vec_bc = [const.tile([P, D], F32, name="vec_bc_%d" % k) for k in range(3)]
-        bo_bc, gamma_bc, beta_bc = vec_bc
-
-        def spread_vectors():
-            for k in range(3):
-                vec_ps = psum_t.tile([P, D], F32, tag="tp")
-                nc.tensor.matmul(out=vec_ps[:], lhsT=ones[:], rhs=vec_rows[:, k, :], start=True, stop=True)
-                nc.scalar.copy(out=vec_bc[k][:], in_=vec_ps[:])
 
         pz_codes = [
             [weights.tile([P, D], U32, name="pz_codes_%d_%d" % (m, g), align_bytes=64) for g in range(2)]
@@ -201,20 +223,18 @@ def tile_softmaxattention_pb_kernel(tc, attn, pz, Wo, bo, x, gamma, beta, out):
             passes = key_passes(j)
             units = HEADS * passes
             grouped = stage.tile([P, units * K_PASS], BF16, tag="att_grouped", align_bytes=64)
-            words = grouped[:].bitcast(F32).rearrange("p (n t u) -> p n t u", t=P, u=2)
+            pairs = grouped[:].bitcast(F32).rearrange("p (n t u) -> p n t u", t=P, u=2)
             for b in range(units // 2):
                 att_t = psum_t.tile([P, 2, 2, P], F32, tag="tp")
                 for n in range(2):
                     m, g = divmod(2 * b + n, passes)
                     for u in range(2):
-                        k0 = g * K_PASS + u * HALF_PASS
-                        nc.tensor.transpose(
-                            att_t[:, n, u, :],
-                            attn_raw[j][:, m, k0 : k0 + HALF_PASS].bitcast(F32),
-                            ident_f32[:],
-                        )
+                        half = 2 * g + u
+                        keys = slice(half * HALF_PASS, (half + 1) * HALF_PASS)
+                        words = attn_raw[j][:, m, keys].bitcast(F32) if half < half_passes(j) else zero_words[:]
+                        nc.tensor.transpose(att_t[:, n, u, :], words, ident_f32[:])
                 nc.scalar.copy(
-                    out=words[:, 2 * b : 2 * b + 2, :, :], in_=att_t[:].rearrange("p n u t -> p n t u")
+                    out=pairs[:, 2 * b : 2 * b + 2, :, :], in_=att_t[:].rearrange("p n u t -> p n t u")
                 )
             att_grouped[j] = grouped
 
@@ -231,7 +251,7 @@ def tile_softmaxattention_pb_kernel(tc, attn, pz, Wo, bo, x, gamma, beta, out):
 
         def head_matmul(j, m):
             if m == 0:
-                grouped = stage.tile([P, HEADS, P, PACK], BF16, tag="cat_grouped", align_bytes=64)
+                grouped = stage.tile([P, HEADS, P, PACK], BF16, tag="cat_grouped", bufs=3, align_bytes=64)
                 cat_grouped[j] = grouped
             codes, scales = att_q[j]
             passes = key_passes(j)
@@ -263,7 +283,10 @@ def tile_softmaxattention_pb_kernel(tc, attn, pz, Wo, bo, x, gamma, beta, out):
 
         def project(j):
             codes, scales = cat_q[j]
-            y_bank = psum_y.tile([P, D], F32, tag="y_ps")
+            if j < 6:
+                y_bank = psum_y.tile([P, D], F32, tag="y_ps")
+            else:
+                y_bank = psum_t.tile([P, D], F32, tag="tp")
             for m in range(HEADS):
                 nc.tensor.matmul_mx(
                     out=y_bank[:],
@@ -279,6 +302,24 @@ def tile_softmaxattention_pb_kernel(tc, attn, pz, Wo, bo, x, gamma, beta, out):
         def add_bias_to_x(j):
             x_plus_bo = stage.tile([P, D], F32, tag="xb", bufs=4)
             nc.vector.tensor_tensor(out=x_plus_bo[:], in0=x_sb[:, j, :], in1=bo_bc[:], op=ALU.add)
+            xb[j] = x_plus_bo
+
+        def add_bias_to_x_on_tensor(j):
+            x_ps = psum_t.tile([P, D], F32, tag="tp")
+            for r in range(VEC_ROWS):
+                cols = slice(r * P, (r + 1) * P)
+                nc.tensor.matmul(
+                    out=x_ps[:, cols], lhsT=ident_bf16[:], rhs=x_sb[:, j, cols], start=True, stop=False
+                )
+                nc.tensor.matmul(
+                    out=x_ps[:, cols],
+                    lhsT=ident_bf16[:, r : r + 1].to_broadcast([P, P]),
+                    rhs=vec_rows[:],
+                    start=False,
+                    stop=True,
+                )
+            x_plus_bo = stage.tile([P, D], F32, tag="xb", bufs=4)
+            nc.scalar.copy(out=x_plus_bo[:], in_=x_ps[:])
             xb[j] = x_plus_bo
 
         def residual(j):
@@ -330,9 +371,8 @@ def tile_softmaxattention_pb_kernel(tc, attn, pz, Wo, bo, x, gamma, beta, out):
             )
             nc.sync.dma_start(out=out[0, j * P : (j + 1) * P, :], in_=result[:])
 
-        ctx.enter_context(tc.manual_schedule())
-        transpose_attn(0)
         spread_vectors()
+        transpose_attn(0)
         transpose_attn(1)
         regroup_pz(0, 0)
         quantise_pz(0, 0)
@@ -344,20 +384,19 @@ def tile_softmaxattention_pb_kernel(tc, attn, pz, Wo, bo, x, gamma, beta, out):
         regroup_pz(2, 0)
         quantise_attn(1)
         quantise_pz(2, 0)
-        head_matmul(1, 0)
         head_matmul(0, 1)
+        head_matmul(1, 0)
         head_matmul(1, 1)
         regroup_pz(3, 0)
         quantise_wo(0)
         quantise_pz(3, 0)
-        transpose_wo(1)
         head_matmul(0, 2)
+        transpose_wo(1)
         head_matmul(1, 2)
         add_bias_to_x(0)
         add_bias_to_x(1)
         quantise_wo(1)
         add_bias_to_x(2)
-        add_bias_to_x(3)
         transpose_attn(2)
         head_matmul(0, 3)
         head_matmul(1, 3)
@@ -375,7 +414,7 @@ def tile_softmaxattention_pb_kernel(tc, attn, pz, Wo, bo, x, gamma, beta, out):
         for r in range(2, TILES + 2):
             if r <= HEADS:
                 regroup_pz(r - 1, 1)
-            if 4 <= r + 1 < TILES:
+            if HEADS <= r < TILES - 1:
                 add_bias_to_x(r + 1)
             if r <= HEADS:
                 quantise_pz(r - 1, 1)
@@ -390,16 +429,16 @@ def tile_softmaxattention_pb_kernel(tc, attn, pz, Wo, bo, x, gamma, beta, out):
                     inverse_std(r - 3)
             if 4 <= r + 2 < TILES:
                 transpose_attn(r + 2)
+            if r < HEADS:
+                add_bias_to_x_on_tensor(r + 1)
             if r + 1 < TILES:
                 quantise_attn(r + 1)
-            if 6 <= r <= TILES:
+            if 2 < r <= TILES:
                 quantise_cat(r - 1)
             residual(r - 2)
             negate_mean(r - 2)
             if r >= 3:
                 finish(r - 3)
-            if 2 < r < 6:
-                quantise_cat(r - 1)
             if r < TILES + 1:
                 centre(r - 2)
         deviation(TILES - 1)

@@ -47,8 +47,8 @@ def tile_softmaxattention_pb_kernel(tc, attn, pz, Wo, bo, x, gamma, beta, out):
         weights = ctx.enter_context(tc.tile_pool(name="weights", bufs=1))
         stage = ctx.enter_context(tc.tile_pool(name="stage", bufs=2))
         stats = ctx.enter_context(tc.tile_pool(name="stats", bufs=3))
-        psum_t = ctx.enter_context(tc.psum_pool(name="psum_t", bufs=4))
-        psum_cat = ctx.enter_context(tc.psum_pool(name="psum_cat", bufs=3))
+        psum_t = ctx.enter_context(tc.psum_pool(name="psum_t", bufs=3))
+        psum_cat = ctx.enter_context(tc.psum_pool(name="psum_cat", bufs=HEADS))
         psum_y = ctx.enter_context(tc.psum_pool(name="psum_y", bufs=1))
 
         ctx.enter_context(tc.manual_schedule())
@@ -219,12 +219,16 @@ def tile_softmaxattention_pb_kernel(tc, attn, pz, Wo, bo, x, gamma, beta, out):
         rstd = {}
         centred = {}
 
-        def transpose_attn(j):
+        def transpose_attn(j, banks=None):
             passes = key_passes(j)
             units = HEADS * passes
-            grouped = stage.tile([P, units * K_PASS], BF16, tag="att_grouped", align_bytes=64)
-            pairs = grouped[:].bitcast(F32).rearrange("p (n t u) -> p n t u", t=P, u=2)
-            for b in range(units // 2):
+            if banks is None:
+                banks = range(units // 2)
+            if banks[0] == 0:
+                grouped = stage.tile([P, units * K_PASS], BF16, tag="att_grouped", align_bytes=64)
+                att_grouped[j] = grouped
+            pairs = att_grouped[j][:].bitcast(F32).rearrange("p (n t u) -> p n t u", t=P, u=2)
+            for b in banks:
                 att_t = psum_t.tile([P, 2, 2, P], F32, tag="tp")
                 for n in range(2):
                     m, g = divmod(2 * b + n, passes)
@@ -236,7 +240,6 @@ def tile_softmaxattention_pb_kernel(tc, attn, pz, Wo, bo, x, gamma, beta, out):
                 nc.scalar.copy(
                     out=pairs[:, 2 * b : 2 * b + 2, :, :], in_=att_t[:].rearrange("p n u t -> p n t u")
                 )
-            att_grouped[j] = grouped
 
         def quantise_attn(j):
             units = HEADS * key_passes(j)
@@ -397,6 +400,7 @@ def tile_softmaxattention_pb_kernel(tc, attn, pz, Wo, bo, x, gamma, beta, out):
         add_bias_to_x(1)
         quantise_wo(1)
         add_bias_to_x(2)
+        add_bias_to_x(3)
         transpose_attn(2)
         head_matmul(0, 3)
         head_matmul(1, 3)
@@ -427,10 +431,10 @@ def tile_softmaxattention_pb_kernel(tc, attn, pz, Wo, bo, x, gamma, beta, out):
                     head_matmul(r, m)
                 if m == 1 and r >= 3:
                     inverse_std(r - 3)
-            if 4 <= r + 2 < TILES:
-                transpose_attn(r + 2)
-            if r < HEADS:
-                add_bias_to_x_on_tensor(r + 1)
+                if m % 2 == 1 and r + 2 < TILES:
+                    transpose_attn(r + 2, range(m - 1, m + 1))
+            if r == 3:
+                add_bias_to_x_on_tensor(4)
             if r + 1 < TILES:
                 quantise_attn(r + 1)
             if 2 < r <= TILES:

@@ -48,8 +48,9 @@ def tile_softmaxattention_pb_kernel(tc, attn, pz, Wo, bo, x, gamma, beta, out):
         stage = ctx.enter_context(tc.tile_pool(name="stage", bufs=2))
         stats = ctx.enter_context(tc.tile_pool(name="stats", bufs=3))
         psum_t = ctx.enter_context(tc.psum_pool(name="psum_t", bufs=3))
-        psum_cat = ctx.enter_context(tc.psum_pool(name="psum_cat", bufs=HEADS))
+        psum_cat = ctx.enter_context(tc.psum_pool(name="psum_cat", bufs=3))
         psum_y = ctx.enter_context(tc.psum_pool(name="psum_y", bufs=1))
+        psum_vec = ctx.enter_context(tc.psum_pool(name="psum_vec", bufs=1))
 
         ctx.enter_context(tc.manual_schedule())
 
@@ -70,8 +71,8 @@ def tile_softmaxattention_pb_kernel(tc, attn, pz, Wo, bo, x, gamma, beta, out):
         nc.vector.tensor_copy(out=ident_bf16[:], in_=ident_f32[:])
         warm = const.tile([P, 1], F32)
         nc.scalar.activation(out=warm[:], in_=eps_col[:], func=ACT.Abs_reciprocal_sqrt)
-        vec_bc = [const.tile([P, D], F32, name="vec_bc_%d" % k) for k in range(3)]
-        bo_bc, gamma_bc, beta_bc = vec_bc
+        bo_bc = const.tile([P, D], F32)
+        gamma_beta = psum_vec.tile([P, 2, D], BF16)
 
         def spread_row(out_ps, k, r):
             row = k * VEC_ROWS + r
@@ -84,17 +85,22 @@ def tile_softmaxattention_pb_kernel(tc, attn, pz, Wo, bo, x, gamma, beta, out):
             )
 
         def spread_vectors():
-            for k in range(3):
-                vec_ps = psum_t.tile([P, D], F32, tag="tp")
+            bo_ps = psum_t.tile([P, D], F32, tag="tp")
+            for r in range(VEC_ROWS):
+                spread_row(bo_ps, 0, r)
+            nc.scalar.copy(out=bo_bc[:], in_=bo_ps[:])
+            for k in range(2):
                 for r in range(VEC_ROWS):
-                    spread_row(vec_ps, k, r)
-                nc.scalar.copy(out=vec_bc[k][:], in_=vec_ps[:])
+                    spread_row(gamma_beta[:, k, :], 1 + k, r)
 
         pz_raw = [
             [inputs.tile([P, PACK, D], BF16, name="pz_raw_%d_%d" % (m, g)) for g in range(2)]
             for m in range(HEADS)
         ]
-        wo_raw = [inputs.tile([P, PACK, K_PASS], BF16, name="wo_raw_%d" % m) for m in range(HEADS)]
+        wo_raw = [
+            [inputs.tile([P, 2, 2 * K_PASS], BF16, name="wo_raw_%d_%d" % (pair, half)) for half in range(2)]
+            for pair in range(2)
+        ]
         attn_raw = [
             inputs.tile([P, HEADS, half_passes(j) * HALF_PASS], BF16, name="attn_raw_%d" % j)
             for j in range(TILES)
@@ -109,10 +115,12 @@ def tile_softmaxattention_pb_kernel(tc, attn, pz, Wo, bo, x, gamma, beta, out):
                 ),
             )
 
-        def load_wo(m):
+        def load_wo(pair, half):
             nc.sync.dma_start(
-                out=wo_raw[m][:],
-                in_=Wo[:, m * K_PASS : (m + 1) * K_PASS].rearrange("(r q) c -> q r c", q=P),
+                out=wo_raw[pair][half][:],
+                in_=Wo[half * 2 * P : (half + 1) * 2 * P, pair * 2 * K_PASS : (pair + 1) * 2 * K_PASS].rearrange(
+                    "(r q) c -> q r c", q=P
+                ),
             )
 
         def load_attn(j):
@@ -136,23 +144,23 @@ def tile_softmaxattention_pb_kernel(tc, attn, pz, Wo, bo, x, gamma, beta, out):
         load_pz(1, 0)
         load_attn(1)
         load_pz(2, 0)
-        load_wo(0)
+        load_wo(0, 0)
         load_pz(3, 0)
-        load_wo(1)
-        load_x(0)
+        load_wo(0, 1)
         load_attn(2)
-        load_wo(2)
-        load_wo(3)
-        load_pz(0, 1)
+        load_x(0)
+        load_wo(1, 0)
+        load_wo(1, 1)
         load_attn(3)
+        load_pz(0, 1)
         load_pz(1, 1)
         load_attn(4)
         load_pz(2, 1)
         load_attn(5)
         load_pz(3, 1)
-        load_x(1)
         load_attn(6)
         load_attn(7)
+        load_x(1)
 
         pz_codes = [
             [weights.tile([P, D], U32, name="pz_codes_%d_%d" % (m, g), align_bytes=64) for g in range(2)]
@@ -182,22 +190,24 @@ def tile_softmaxattention_pb_kernel(tc, attn, pz, Wo, bo, x, gamma, beta, out):
                 in_=pz_grouped[(m, g)][:],
             )
 
-        def transpose_wo(m):
-            grouped = stage.tile([P, D * PACK], BF16, tag="wo_grouped", align_bytes=64)
-            words = grouped[:].bitcast(F32).rearrange("p (r q u) -> p r q u", q=P, u=2)
-            for half in range(2):
+        def transpose_wo(pair, half):
+            for m in (2 * pair, 2 * pair + 1):
+                if half == 0:
+                    grouped = stage.tile([P, D * PACK], BF16, tag="wo_grouped", align_bytes=64)
+                    wo_grouped[m] = grouped
+                words = wo_grouped[m][:].bitcast(F32).rearrange("p (r q u) -> p r q u", q=P, u=2)
                 wo_t = psum_t.tile([P, 2, 2, P], F32, tag="tp")
                 for r in range(2):
                     for u in range(2):
+                        c0 = (m % 2) * K_PASS + u * HALF_PASS
                         nc.tensor.transpose(
                             wo_t[:, r, u, :],
-                            wo_raw[m][:, 2 * half + r, u * HALF_PASS : (u + 1) * HALF_PASS].bitcast(F32),
+                            wo_raw[pair][half][:, r, c0 : c0 + HALF_PASS].bitcast(F32),
                             ident_f32[:],
                         )
                 nc.scalar.copy(
                     out=words[:, 2 * half : 2 * half + 2, :, :], in_=wo_t[:].rearrange("p r u q -> p r q u")
                 )
-            wo_grouped[m] = grouped
 
         def quantise_wo(m):
             nc.vector.quantize_mx(
@@ -302,27 +312,9 @@ def tile_softmaxattention_pb_kernel(tc, attn, pz, Wo, bo, x, gamma, beta, out):
                 )
             y_ps[j] = y_bank
 
-        def add_bias_to_x(j):
+        def add_bias_to_x(j, engine):
             x_plus_bo = stage.tile([P, D], F32, tag="xb", bufs=4)
-            nc.vector.tensor_tensor(out=x_plus_bo[:], in0=x_sb[:, j, :], in1=bo_bc[:], op=ALU.add)
-            xb[j] = x_plus_bo
-
-        def add_bias_to_x_on_tensor(j):
-            x_ps = psum_t.tile([P, D], F32, tag="tp")
-            for r in range(VEC_ROWS):
-                cols = slice(r * P, (r + 1) * P)
-                nc.tensor.matmul(
-                    out=x_ps[:, cols], lhsT=ident_bf16[:], rhs=x_sb[:, j, cols], start=True, stop=False
-                )
-                nc.tensor.matmul(
-                    out=x_ps[:, cols],
-                    lhsT=ident_bf16[:, r : r + 1].to_broadcast([P, P]),
-                    rhs=vec_rows[:],
-                    start=False,
-                    stop=True,
-                )
-            x_plus_bo = stage.tile([P, D], F32, tag="xb", bufs=4)
-            nc.scalar.copy(out=x_plus_bo[:], in_=x_ps[:])
+            engine.tensor_tensor(out=x_plus_bo[:], in0=x_sb[:, j, :], in1=bo_bc[:], op=ALU.add)
             xb[j] = x_plus_bo
 
         def residual(j):
@@ -361,7 +353,7 @@ def tile_softmaxattention_pb_kernel(tc, attn, pz, Wo, bo, x, gamma, beta, out):
         def centre(j):
             scaled = stage.tile([P, D], F32, tag="centred")
             nc.vector.scalar_tensor_tensor(
-                out=scaled[:], in0=h[j][:], scalar=negmean[j][:], in1=gamma_bc[:],
+                out=scaled[:], in0=h[j][:], scalar=negmean[j][:], in1=gamma_beta[:, 0, :],
                 op0=ALU.add, op1=ALU.mult,
             )
             centred[j] = scaled
@@ -369,7 +361,7 @@ def tile_softmaxattention_pb_kernel(tc, attn, pz, Wo, bo, x, gamma, beta, out):
         def finish(j):
             result = stage.tile([P, D], F32, tag="result")
             nc.vector.scalar_tensor_tensor(
-                out=result[:], in0=centred[j][:], scalar=rstd[j][:], in1=beta_bc[:],
+                out=result[:], in0=centred[j][:], scalar=rstd[j][:], in1=gamma_beta[:, 1, :],
                 op0=ALU.mult, op1=ALU.add,
             )
             nc.sync.dma_start(out=out[0, j * P : (j + 1) * P, :], in_=result[:])
@@ -383,7 +375,7 @@ def tile_softmaxattention_pb_kernel(tc, attn, pz, Wo, bo, x, gamma, beta, out):
         quantise_attn(0)
         quantise_pz(1, 0)
         head_matmul(0, 0)
-        transpose_wo(0)
+        transpose_wo(0, 0)
         regroup_pz(2, 0)
         quantise_attn(1)
         quantise_pz(2, 0)
@@ -391,21 +383,20 @@ def tile_softmaxattention_pb_kernel(tc, attn, pz, Wo, bo, x, gamma, beta, out):
         head_matmul(1, 0)
         head_matmul(1, 1)
         regroup_pz(3, 0)
-        quantise_wo(0)
         quantise_pz(3, 0)
         head_matmul(0, 2)
-        transpose_wo(1)
+        transpose_wo(0, 1)
         head_matmul(1, 2)
-        add_bias_to_x(0)
-        add_bias_to_x(1)
+        add_bias_to_x(0, nc.vector)
+        add_bias_to_x(1, nc.vector)
+        quantise_wo(0)
         quantise_wo(1)
-        add_bias_to_x(2)
-        add_bias_to_x(3)
+        add_bias_to_x(2, nc.vector)
         transpose_attn(2)
         head_matmul(0, 3)
         head_matmul(1, 3)
-        transpose_wo(2)
-        transpose_wo(3)
+        transpose_wo(1, 0)
+        transpose_wo(1, 1)
         quantise_cat(0)
         quantise_attn(2)
         quantise_cat(1)
@@ -418,10 +409,16 @@ def tile_softmaxattention_pb_kernel(tc, attn, pz, Wo, bo, x, gamma, beta, out):
         for r in range(2, TILES + 2):
             if r <= HEADS:
                 regroup_pz(r - 1, 1)
-            if HEADS <= r < TILES - 1:
-                add_bias_to_x(r + 1)
+            if r == 3:
+                quantise_attn(r + 1)
+            elif 2 < r <= TILES:
+                quantise_cat(r - 1)
             if r <= HEADS:
                 quantise_pz(r - 1, 1)
+            if r == 3:
+                quantise_cat(r - 1)
+            elif r + 1 < TILES:
+                quantise_attn(r + 1)
             for m in range(HEADS):
                 if m == 1 and r >= 3:
                     deviation(r - 3)
@@ -431,16 +428,14 @@ def tile_softmaxattention_pb_kernel(tc, attn, pz, Wo, bo, x, gamma, beta, out):
                     head_matmul(r, m)
                 if m == 1 and r >= 3:
                     inverse_std(r - 3)
-                if m % 2 == 1 and r + 2 < TILES:
+                if m % 2 == 1 and 3 <= r < TILES - 2:
                     transpose_attn(r + 2, range(m - 1, m + 1))
-            if r == 3:
-                add_bias_to_x_on_tensor(4)
-            if r + 1 < TILES:
-                quantise_attn(r + 1)
-            if 2 < r <= TILES:
-                quantise_cat(r - 1)
+            if r == 2:
+                transpose_attn(r + 2)
             residual(r - 2)
             negate_mean(r - 2)
+            if r + 1 < TILES:
+                add_bias_to_x(r + 1, nc.gpsimd)
             if r >= 3:
                 finish(r - 3)
             if r < TILES + 1:

@@ -147,20 +147,20 @@ def tile_softmaxattention_pb_kernel(tc, attn, pz, Wo, bo, x, gamma, beta, out):
         load_wo(0, 0)
         load_pz(3, 0)
         load_wo(0, 1)
-        load_attn(2)
         load_x(0)
+        load_attn(2)
         load_wo(1, 0)
         load_wo(1, 1)
-        load_attn(3)
         load_pz(0, 1)
+        load_attn(3)
         load_pz(1, 1)
         load_attn(4)
         load_pz(2, 1)
         load_attn(5)
         load_pz(3, 1)
         load_attn(6)
-        load_attn(7)
         load_x(1)
+        load_attn(7)
 
         pz_codes = [
             [weights.tile([P, D], U32, name="pz_codes_%d_%d" % (m, g), align_bytes=64) for g in range(2)]
@@ -392,16 +392,16 @@ def tile_softmaxattention_pb_kernel(tc, attn, pz, Wo, bo, x, gamma, beta, out):
         quantise_wo(0)
         quantise_wo(1)
         add_bias_to_x(2, nc.vector)
-        transpose_attn(2)
         head_matmul(0, 3)
         head_matmul(1, 3)
+        transpose_attn(2)
         transpose_wo(1, 0)
         transpose_wo(1, 1)
         quantise_cat(0)
-        quantise_attn(2)
         quantise_cat(1)
-        quantise_wo(2)
+        quantise_attn(2)
         regroup_pz(0, 1)
+        quantise_wo(2)
         quantise_wo(3)
         quantise_pz(0, 1)
         transpose_attn(3)
@@ -409,24 +409,24 @@ def tile_softmaxattention_pb_kernel(tc, attn, pz, Wo, bo, x, gamma, beta, out):
         for r in range(2, TILES + 2):
             if r <= HEADS:
                 regroup_pz(r - 1, 1)
-            if r == 3:
+            if r <= 3:
                 quantise_attn(r + 1)
-            elif 2 < r <= TILES:
+            elif r <= TILES:
                 quantise_cat(r - 1)
             if r <= HEADS:
                 quantise_pz(r - 1, 1)
             if r == 3:
                 quantise_cat(r - 1)
-            elif r + 1 < TILES:
+            elif 3 < r < TILES - 1:
                 quantise_attn(r + 1)
             for m in range(HEADS):
-                if m == 1 and r >= 3:
+                if m == 0 and r >= 3:
                     deviation(r - 3)
-                if m == 2:
+                if m == (3 if r == 2 else 2):
                     project(r - 2)
                 if r < TILES:
                     head_matmul(r, m)
-                if m == 1 and r >= 3:
+                if m == 0 and r >= 3:
                     inverse_std(r - 3)
                 if m % 2 == 1 and 3 <= r < TILES - 2:
                     transpose_attn(r + 2, range(m - 1, m + 1))

@@ -284,25 +284,29 @@ def tile_softmaxattention_pb_kernel(tc, attn, pz, Wo, bo, x, gamma, beta, out):
                     )
             nc.scalar.copy(out=cat_grouped[j][:, m, :, :], in_=cat_ps[:].rearrange("p a t -> p t a"))
 
-        def quantise_cat(j):
-            codes = stage.tile([P, HEADS, P], U32, tag="cat_codes", align_bytes=64)
-            scales = stage.tile([P, HEADS, P], U8, tag="cat_scales", align_bytes=64)
+        def quantise_cat(j, heads=range(HEADS)):
+            if heads[0] == 0:
+                codes = stage.tile([P, HEADS, P], U32, tag="cat_codes", align_bytes=64)
+                scales = stage.tile([P, HEADS, P], U8, tag="cat_scales", align_bytes=64)
+                cat_q[j] = (codes, scales)
+            part = slice(heads[0], heads[-1] + 1)
             nc.vector.quantize_mx(
-                out=codes[:].rearrange("p m t -> p (m t)").bitcast(FP8X4),
-                scales=scales[:].rearrange("p m t -> p (m t)"),
-                in_=cat_grouped[j][:].rearrange("p m t a -> p (m t a)"),
+                out=cat_q[j][0][:, part, :].rearrange("p m t -> p (m t)").bitcast(FP8X4),
+                scales=cat_q[j][1][:, part, :].rearrange("p m t -> p (m t)"),
+                in_=cat_grouped[j][:, part, :, :].rearrange("p m t a -> p (m t a)"),
             )
-            cat_q[j] = (codes, scales)
 
-        def project(j):
+        def project(j, heads=range(HEADS)):
             codes, scales = cat_q[j]
-            if j < 6:
-                y_bank = psum_y.tile([P, D], F32, tag="y_ps")
-            else:
-                y_bank = psum_t.tile([P, D], F32, tag="tp")
-            for m in range(HEADS):
+            if heads[0] == 0:
+                if j < 6:
+                    y_bank = psum_y.tile([P, D], F32, tag="y_ps")
+                else:
+                    y_bank = psum_t.tile([P, D], F32, tag="tp")
+                y_ps[j] = y_bank
+            for m in heads:
                 nc.tensor.matmul_mx(
-                    out=y_bank[:],
+                    out=y_ps[j][:],
                     lhsT=codes[:, m, :].bitcast(FP8X4),
                     lhsT_scale=scales[:, m, :],
                     rhs=wo_codes[m][:].bitcast(FP8X4),
@@ -310,7 +314,6 @@ def tile_softmaxattention_pb_kernel(tc, attn, pz, Wo, bo, x, gamma, beta, out):
                     start=(m == 0),
                     stop=(m == HEADS - 1),
                 )
-            y_ps[j] = y_bank
 
         def add_bias_to_x(j, engine):
             x_plus_bo = stage.tile([P, D], F32, tag="xb", bufs=4)
@@ -318,7 +321,7 @@ def tile_softmaxattention_pb_kernel(tc, attn, pz, Wo, bo, x, gamma, beta, out):
             xb[j] = x_plus_bo
 
         def residual(j):
-            h_tile = stage.tile([P, D], F32, tag="h")
+            h_tile = stage.tile([P, D], F32, tag="h", bufs=3)
             row_sum = stats.tile([P, 1], F32, tag="hsum")
             nc.vector.scalar_tensor_tensor(
                 out=h_tile[:], in0=y_ps[j][:], scalar=1.0, in1=xb[j][:], op0=ALU.mult, op1=ALU.add,
@@ -351,20 +354,23 @@ def tile_softmaxattention_pb_kernel(tc, attn, pz, Wo, bo, x, gamma, beta, out):
             rstd[j] = inv_std
 
         def centre(j):
-            scaled = stage.tile([P, D], F32, tag="centred")
+            scaled = stage.tile([P, D], F32, tag="centred", bufs=3)
             nc.vector.scalar_tensor_tensor(
                 out=scaled[:], in0=h[j][:], scalar=negmean[j][:], in1=gamma_beta[:, 0, :],
                 op0=ALU.add, op1=ALU.mult,
             )
             centred[j] = scaled
 
-        def finish(j):
+        def finish(j, queues):
             result = stage.tile([P, D], F32, tag="result")
-            nc.vector.scalar_tensor_tensor(
-                out=result[:], in0=centred[j][:], scalar=rstd[j][:], in1=gamma_beta[:, 1, :],
-                op0=ALU.mult, op1=ALU.add,
-            )
-            nc.sync.dma_start(out=out[0, j * P : (j + 1) * P, :], in_=result[:])
+            width = D // len(queues)
+            for n, queue in enumerate(queues):
+                cols = slice(n * width, (n + 1) * width)
+                nc.vector.scalar_tensor_tensor(
+                    out=result[:, cols], in0=centred[j][:, cols], scalar=rstd[j][:], in1=gamma_beta[:, 1, cols],
+                    op0=ALU.mult, op1=ALU.add,
+                )
+                queue.dma_start(out=out[0, j * P : (j + 1) * P, cols], in_=result[:, cols])
 
         spread_vectors()
         transpose_attn(0)
@@ -406,12 +412,12 @@ def tile_softmaxattention_pb_kernel(tc, attn, pz, Wo, bo, x, gamma, beta, out):
         quantise_pz(0, 1)
         transpose_attn(3)
 
-        for r in range(2, TILES + 2):
+        for r in range(2, TILES):
             if r <= HEADS:
                 regroup_pz(r - 1, 1)
             if r <= 3:
                 quantise_attn(r + 1)
-            elif r <= TILES:
+            else:
                 quantise_cat(r - 1)
             if r <= HEADS:
                 quantise_pz(r - 1, 1)
@@ -419,15 +425,16 @@ def tile_softmaxattention_pb_kernel(tc, attn, pz, Wo, bo, x, gamma, beta, out):
                 quantise_cat(r - 1)
             elif 3 < r < TILES - 1:
                 quantise_attn(r + 1)
+            if r >= 3:
+                deviation(r - 3)
             for m in range(HEADS):
-                if m == 0 and r >= 3:
-                    deviation(r - 3)
-                if m == (3 if r == 2 else 2):
+                if r == 2 and m == 3:
                     project(r - 2)
-                if r < TILES:
-                    head_matmul(r, m)
-                if m == 0 and r >= 3:
+                head_matmul(r, m)
+                if r >= 3 and m == 0:
                     inverse_std(r - 3)
+                if r >= 3 and m == 1:
+                    project(r - 2)
                 if m % 2 == 1 and 3 <= r < TILES - 2:
                     transpose_attn(r + 2, range(m - 1, m + 1))
             if r == 2:
@@ -436,11 +443,28 @@ def tile_softmaxattention_pb_kernel(tc, attn, pz, Wo, bo, x, gamma, beta, out):
             negate_mean(r - 2)
             if r + 1 < TILES:
                 add_bias_to_x(r + 1, nc.gpsimd)
+            if r == TILES - 1:
+                quantise_cat(r, range(0, 2))
             if r >= 3:
-                finish(r - 3)
-            if r < TILES + 1:
-                centre(r - 2)
-        deviation(TILES - 1)
-        inverse_std(TILES - 1)
-        centre(TILES - 1)
-        finish(TILES - 1)
+                finish(r - 3, [nc.sync])
+            centre(r - 2)
+
+        deviation(5)
+        inverse_std(5)
+        project(6)
+        project(7, range(0, 2))
+        quantise_cat(7, range(2, HEADS))
+        project(7, range(2, HEADS))
+        residual(6)
+        negate_mean(6)
+        finish(5, [nc.sync])
+        residual(7)
+        negate_mean(7)
+        deviation(6)
+        inverse_std(6)
+        deviation(7)
+        inverse_std(7)
+        centre(6)
+        centre(7)
+        finish(6, [nc.sync])
+        finish(7, [nc.sync, nc.scalar])

from contextlib import ExitStack

import concourse.mybir as mybir
from concourse.masks import make_identity

F32 = mybir.dt.float32
BF16 = mybir.dt.bfloat16
U32 = mybir.dt.uint32
U8 = mybir.dt.uint8
FP8X4 = mybir.dt.float8_e4m3fn_x4
ALU = mybir.AluOpType
ACT = mybir.ActivationFunctionType

P = 128
PACK = 4
K_PASS = P * PACK
HALF_PASS = K_PASS // 2
HEADS = 4
T = 1024
D = 512
TILES = T // P
VEC_ROWS = D // P
CAUSAL_BLOCK = 512
LN_EPS = 1e-5

FLOPS = 2 * HEADS * D * (CAUSAL_BLOCK * CAUSAL_BLOCK + CAUSAL_BLOCK * T) + 2 * T * HEADS * D * D
BYTES = 2 * (HEADS * T * (T + 1) // 2 + HEADS * T * D + D * HEADS * D + T * D + 3 * D) + 4 * T * D


def key_passes(j):
    return (j * P) // CAUSAL_BLOCK + 1


def half_passes(j):
    return -(-seen_keys(j) // HALF_PASS)


def seen_keys(j):
    return (j + 1) * P


def tile_softmaxattention_pb_kernel(tc, attn, pz, Wo, bo, x, gamma, beta, out):
    nc = tc.nc
    with ExitStack() as ctx:
        inputs = ctx.enter_context(tc.tile_pool(name="inputs", bufs=1))
        const = ctx.enter_context(tc.tile_pool(name="const", bufs=1))
        weights = ctx.enter_context(tc.tile_pool(name="weights", bufs=1))
        stage = ctx.enter_context(tc.tile_pool(name="stage", bufs=2))
        stats = ctx.enter_context(tc.tile_pool(name="stats", bufs=3))
        psum_t = ctx.enter_context(tc.psum_pool(name="psum_t", bufs=3))
        psum_cat = ctx.enter_context(tc.psum_pool(name="psum_cat", bufs=3))
        psum_y = ctx.enter_context(tc.psum_pool(name="psum_y", bufs=1))
        psum_vec = ctx.enter_context(tc.psum_pool(name="psum_vec", bufs=1))

        ctx.enter_context(tc.manual_schedule())

        ident_f32 = const.tile([P, P], F32)
        make_identity(nc, ident_f32[:])
        zero_words = const.tile([P, P], F32)
        nc.gpsimd.memset(zero_words[:], 0.0)

        vec_rows = const.tile([P, P], BF16)
        nc.vector.memset(vec_rows[:].bitcast(F32), 0.0)
        for k, vec in enumerate((bo, gamma, beta)):
            nc.scalar.dma_start(
                out=vec_rows[k * VEC_ROWS : (k + 1) * VEC_ROWS, :], in_=vec.rearrange("(r n) -> r n", n=P)
            )
        eps_col = const.tile([P, 1], F32)
        nc.vector.memset(eps_col[:], LN_EPS)
        ident_bf16 = const.tile([P, P], BF16)
        nc.vector.tensor_copy(out=ident_bf16[:], in_=ident_f32[:])
        warm = const.tile([P, 1], F32)
        nc.scalar.activation(out=warm[:], in_=eps_col[:], func=ACT.Abs_reciprocal_sqrt)
        bo_bc = const.tile([P, D], F32)
        gamma_beta = psum_vec.tile([P, 2, D], BF16)

        def spread_row(out_ps, k, r):
            row = k * VEC_ROWS + r
            nc.tensor.matmul(
                out=out_ps[:, r * P : (r + 1) * P],
                lhsT=ident_bf16[:, row : row + 1].to_broadcast([P, P]),
                rhs=vec_rows[:],
                start=True,
                stop=True,
            )

        def spread_vectors():
            bo_ps = psum_t.tile([P, D], F32, tag="tp")
            for r in range(VEC_ROWS):
                spread_row(bo_ps, 0, r)
            nc.scalar.copy(out=bo_bc[:], in_=bo_ps[:])
            for k in range(2):
                for r in range(VEC_ROWS):
                    spread_row(gamma_beta[:, k, :], 1 + k, r)

        pz_raw = [
            [inputs.tile([P, PACK, D], BF16, name="pz_raw_%d_%d" % (m, g)) for g in range(2)]
            for m in range(HEADS)
        ]
        wo_raw = [
            [inputs.tile([P, 2, 2 * K_PASS], BF16, name="wo_raw_%d_%d" % (pair, half)) for half in range(2)]
            for pair in range(2)
        ]
        attn_raw = [
            inputs.tile([P, HEADS, half_passes(j) * HALF_PASS], BF16, name="attn_raw_%d" % j)
            for j in range(TILES)
        ]
        x_sb = inputs.tile([P, TILES, D], BF16)

        def load_pz(m, g):
            nc.sync.dma_start(
                out=pz_raw[m][g][:].rearrange("p (u e) i -> p u (e i)", u=2),
                in_=pz[0, m, g * K_PASS : (g + 1) * K_PASS, :].rearrange(
                    "(u p e) i -> p u (e i)", u=2, e=2
                ),
            )

        def load_wo(pair, half):
            nc.sync.dma_start(
                out=wo_raw[pair][half][:],
                in_=Wo[half * 2 * P : (half + 1) * 2 * P, pair * 2 * K_PASS : (pair + 1) * 2 * K_PASS].rearrange(
                    "(r q) c -> q r c", q=P
                ),
            )

        def load_attn(j):
            keys = seen_keys(j)
            if keys < half_passes(j) * HALF_PASS:
                nc.gpsimd.memset(attn_raw[j][:, :, keys:].bitcast(F32), 0.0)
            nc.sync.dma_start(
                out=attn_raw[j][:, :, 0:keys],
                in_=attn[0, :, j * P : (j + 1) * P, 0:keys].rearrange("m p s -> p m s"),
            )

        def load_x(half):
            tiles = slice(half * TILES // 2, (half + 1) * TILES // 2)
            rows = slice(half * T // 2, (half + 1) * T // 2)
            nc.sync.dma_start(
                out=x_sb[:, tiles, :], in_=x[0, rows, :].rearrange("(j p) o -> p j o", p=P)
            )

        load_pz(0, 0)
        load_attn(0)
        load_pz(1, 0)
        load_attn(1)
        load_pz(2, 0)
        load_wo(0, 0)
        load_pz(3, 0)
        load_wo(0, 1)
        load_x(0)
        load_attn(2)
        load_wo(1, 0)
        load_wo(1, 1)
        load_pz(0, 1)
        load_attn(3)
        load_pz(1, 1)
        load_attn(4)
        load_pz(2, 1)
        load_attn(5)
        load_pz(3, 1)
        load_attn(6)
        load_x(1)
        load_attn(7)

        pz_codes = [
            [weights.tile([P, D], U32, name="pz_codes_%d_%d" % (m, g), align_bytes=64) for g in range(2)]
            for m in range(HEADS)
        ]
        pz_scales = [
            [weights.tile([P, D], U8, name="pz_scales_%d_%d" % (m, g), align_bytes=64) for g in range(2)]
            for m in range(HEADS)
        ]
        wo_codes = [weights.tile([P, D], U32, name="wo_codes_%d" % m, align_bytes=64) for m in range(HEADS)]
        wo_scales = [weights.tile([P, D], U8, name="wo_scales_%d" % m, align_bytes=64) for m in range(HEADS)]
        pz_grouped = {}
        wo_grouped = {}

        def regroup_pz(m, g):
            grouped = stage.tile([P, D * PACK], BF16, tag="pz_grouped", align_bytes=64)
            nc.vector.tensor_copy(
                out=grouped[:].rearrange("p (e c i k) -> p c k e i", e=2, i=4, k=PACK),
                in_=pz_raw[m][g][:].rearrange("p k (c i e) -> p c k e i", i=4, e=2),
            )
            pz_grouped[(m, g)] = grouped

        def quantise_pz(m, g):
            nc.vector.quantize_mx(
                out=pz_codes[m][g][:].bitcast(FP8X4),
                scales=pz_scales[m][g][:],
                in_=pz_grouped[(m, g)][:],
            )

        def transpose_wo(pair, half):
            for m in (2 * pair, 2 * pair + 1):
                if half == 0:
                    grouped = stage.tile([P, D * PACK], BF16, tag="wo_grouped", align_bytes=64)
                    wo_grouped[m] = grouped
                words = wo_grouped[m][:].bitcast(F32).rearrange("p (r q u) -> p r q u", q=P, u=2)
                wo_t = psum_t.tile([P, 2, 2, P], F32, tag="tp")
                for r in range(2):
                    for u in range(2):
                        c0 = (m % 2) * K_PASS + u * HALF_PASS
                        nc.tensor.transpose(
                            wo_t[:, r, u, :],
                            wo_raw[pair][half][:, r, c0 : c0 + HALF_PASS].bitcast(F32),
                            ident_f32[:],
                        )
                nc.scalar.copy(
                    out=words[:, 2 * half : 2 * half + 2, :, :], in_=wo_t[:].rearrange("p r u q -> p r q u")
                )

        def quantise_wo(m):
            nc.vector.quantize_mx(
                out=wo_codes[m][:].bitcast(FP8X4),
                scales=wo_scales[m][:],
                in_=wo_grouped[m][:],
            )

        att_grouped = {}
        att_q = {}
        cat_grouped = {}
        cat_q = {}
        y_ps = {}
        xb = {}
        h = {}
        hsum = {}
        negmean = {}
        ssqs = {}
        rstd = {}
        centred = {}

        def transpose_attn(j, banks=None):
            passes = key_passes(j)
            units = HEADS * passes
            if banks is None:
                banks = range(units // 2)
            if banks[0] == 0:
                grouped = stage.tile([P, units * K_PASS], BF16, tag="att_grouped", align_bytes=64)
                att_grouped[j] = grouped
            pairs = att_grouped[j][:].bitcast(F32).rearrange("p (n t u) -> p n t u", t=P, u=2)
            for b in banks:
                att_t = psum_t.tile([P, 2, 2, P], F32, tag="tp")
                for n in range(2):
                    m, g = divmod(2 * b + n, passes)
                    for u in range(2):
                        half = 2 * g + u
                        keys = slice(half * HALF_PASS, (half + 1) * HALF_PASS)
                        words = attn_raw[j][:, m, keys].bitcast(F32) if half < half_passes(j) else zero_words[:]
                        nc.tensor.transpose(att_t[:, n, u, :], words, ident_f32[:])
                nc.scalar.copy(
                    out=pairs[:, 2 * b : 2 * b + 2, :, :], in_=att_t[:].rearrange("p n u t -> p n t u")
                )

        def quantise_attn(j):
            units = HEADS * key_passes(j)
            codes = stage.tile([P, units, P], U32, tag="att_codes", bufs=4, align_bytes=64)
            scales = stage.tile([P, units, P], U8, tag="att_scales", bufs=4, align_bytes=64)
            nc.vector.quantize_mx(
                out=codes[:].rearrange("p n t -> p (n t)").bitcast(FP8X4),
                scales=scales[:].rearrange("p n t -> p (n t)"),
                in_=att_grouped[j][:],
            )
            att_q[j] = (codes, scales)

        def head_matmul(j, m):
            if m == 0:
                grouped = stage.tile([P, HEADS, P, PACK], BF16, tag="cat_grouped", bufs=3, align_bytes=64)
                cat_grouped[j] = grouped
            codes, scales = att_q[j]
            passes = key_passes(j)
            cat_ps = psum_cat.tile([P, PACK, P], F32, tag="cat_ps")
            for a in range(PACK):
                u, e = divmod(a, 2)
                cols = slice((2 * e + u) * P, (2 * e + u + 1) * P)
                for g in range(passes):
                    nc.tensor.matmul_mx(
                        out=cat_ps[:, a, :],
                        lhsT=pz_codes[m][g][:, cols].bitcast(FP8X4),
                        lhsT_scale=pz_scales[m][g][:, cols],
                        rhs=codes[:, m * passes + g, :].bitcast(FP8X4),
                        rhs_scale=scales[:, m * passes + g, :],
                        start=(g == 0),
                        stop=(g == passes - 1),
                    )
            nc.scalar.copy(out=cat_grouped[j][:, m, :, :], in_=cat_ps[:].rearrange("p a t -> p t a"))

        def quantise_cat(j, heads=range(HEADS)):
            if heads[0] == 0:
                codes = stage.tile([P, HEADS, P], U32, tag="cat_codes", align_bytes=64)
                scales = stage.tile([P, HEADS, P], U8, tag="cat_scales", align_bytes=64)
                cat_q[j] = (codes, scales)
            part = slice(heads[0], heads[-1] + 1)
            nc.vector.quantize_mx(
                out=cat_q[j][0][:, part, :].rearrange("p m t -> p (m t)").bitcast(FP8X4),
                scales=cat_q[j][1][:, part, :].rearrange("p m t -> p (m t)"),
                in_=cat_grouped[j][:, part, :, :].rearrange("p m t a -> p (m t a)"),
            )

        def project(j, heads=range(HEADS)):
            codes, scales = cat_q[j]
            if heads[0] == 0:
                if j < 6:
                    y_bank = psum_y.tile([P, D], F32, tag="y_ps")
                else:
                    y_bank = psum_t.tile([P, D], F32, tag="tp")
                y_ps[j] = y_bank
            for m in heads:
                nc.tensor.matmul_mx(
                    out=y_ps[j][:],
                    lhsT=codes[:, m, :].bitcast(FP8X4),
                    lhsT_scale=scales[:, m, :],
                    rhs=wo_codes[m][:].bitcast(FP8X4),
                    rhs_scale=wo_scales[m][:],
                    start=(m == 0),
                    stop=(m == HEADS - 1),
                )

        def add_bias_to_x(j, engine):
            x_plus_bo = stage.tile([P, D], F32, tag="xb", bufs=4)
            engine.tensor_tensor(out=x_plus_bo[:], in0=x_sb[:, j, :], in1=bo_bc[:], op=ALU.add)
            xb[j] = x_plus_bo

        def residual(j):
            h_tile = stage.tile([P, D], F32, tag="h", bufs=3)
            row_sum = stats.tile([P, 1], F32, tag="hsum")
            nc.vector.scalar_tensor_tensor(
                out=h_tile[:], in0=y_ps[j][:], scalar=1.0, in1=xb[j][:], op0=ALU.mult, op1=ALU.add,
                accum_out=row_sum[:],
            )
            h[j] = h_tile
            hsum[j] = row_sum

        def negate_mean(j):
            minus_mean = stats.tile([P, 1], F32, tag="negmean")
            nc.gpsimd.tensor_scalar(
                out=minus_mean[:], in0=hsum[j][:], scalar1=-1.0 / D, scalar2=None, op0=ALU.mult
            )
            negmean[j] = minus_mean

        def deviation(j):
            squares = stage.tile([P, D], BF16, tag="squares")
            ssq = stats.tile([P, 1], F32, tag="ssq")
            nc.scalar.activation(
                out=squares[:], in_=h[j][:], func=ACT.Square, bias=negmean[j][:], scale=1.0,
                accum_out=ssq[:],
            )
            ssqs[j] = ssq

        def inverse_std(j):
            inv_std = stats.tile([P, 1], F32, tag="rstd")
            nc.scalar.activation(
                out=inv_std[:], in_=ssqs[j][:], func=ACT.Abs_reciprocal_sqrt, bias=eps_col[:], scale=1.0 / D
            )
            rstd[j] = inv_std

        def centre(j):
            scaled = stage.tile([P, D], F32, tag="centred", bufs=3)
            nc.vector.scalar_tensor_tensor(
                out=scaled[:], in0=h[j][:], scalar=negmean[j][:], in1=gamma_beta[:, 0, :],
                op0=ALU.add, op1=ALU.mult,
            )
            centred[j] = scaled

        def finish(j, queues):
            result = stage.tile([P, D], F32, tag="result")
            width = D // len(queues)
            for n, queue in enumerate(queues):
                cols = slice(n * width, (n + 1) * width)
                nc.vector.scalar_tensor_tensor(
                    out=result[:, cols], in0=centred[j][:, cols], scalar=rstd[j][:], in1=gamma_beta[:, 1, cols],
                    op0=ALU.mult, op1=ALU.add,
                )
                queue.dma_start(out=out[0, j * P : (j + 1) * P, cols], in_=result[:, cols])

        spread_vectors()
        transpose_attn(0)
        transpose_attn(1)
        regroup_pz(0, 0)
        quantise_pz(0, 0)
        regroup_pz(1, 0)
        quantise_attn(0)
        quantise_pz(1, 0)
        head_matmul(0, 0)
        transpose_wo(0, 0)
        regroup_pz(2, 0)
        quantise_attn(1)
        quantise_pz(2, 0)
        head_matmul(0, 1)
        head_matmul(1, 0)
        head_matmul(1, 1)
        regroup_pz(3, 0)
        quantise_pz(3, 0)
        head_matmul(0, 2)
        transpose_wo(0, 1)
        head_matmul(1, 2)
        add_bias_to_x(0, nc.vector)
        add_bias_to_x(1, nc.vector)
        quantise_wo(0)
        quantise_wo(1)
        add_bias_to_x(2, nc.vector)
        head_matmul(0, 3)
        head_matmul(1, 3)
        transpose_attn(2)
        transpose_wo(1, 0)
        transpose_wo(1, 1)
        quantise_cat(0)
        quantise_cat(1)
        quantise_attn(2)
        regroup_pz(0, 1)
        quantise_wo(2)
        quantise_wo(3)
        quantise_pz(0, 1)
        transpose_attn(3)

        for r in range(2, TILES):
            if r <= HEADS:
                regroup_pz(r - 1, 1)
            if r <= 3:
                quantise_attn(r + 1)
            else:
                quantise_cat(r - 1)
            if r <= HEADS:
                quantise_pz(r - 1, 1)
            if r == 3:
                quantise_cat(r - 1)
            elif 3 < r < TILES - 1:
                quantise_attn(r + 1)
            if r >= 3:
                deviation(r - 3)
            for m in range(HEADS):
                if r == 2 and m == 3:
                    project(r - 2)
                head_matmul(r, m)
                if r >= 3 and m == 0:
                    inverse_std(r - 3)
                if r >= 3 and m == 1:
                    project(r - 2)
                if m % 2 == 1 and 3 <= r < TILES - 2:
                    transpose_attn(r + 2, range(m - 1, m + 1))
            if r == 2:
                transpose_attn(r + 2)
            residual(r - 2)
            negate_mean(r - 2)
            if r + 1 < TILES:
                add_bias_to_x(r + 1, nc.gpsimd)
            if r == TILES - 1:
                quantise_cat(r, range(0, 2))
            if r >= 3:
                finish(r - 3, [nc.sync])
            centre(r - 2)

        deviation(5)
        inverse_std(5)
        project(6)
        project(7, range(0, 2))
        quantise_cat(7, range(2, HEADS))
        project(7, range(2, HEADS))
        residual(6)
        negate_mean(6)
        finish(5, [nc.sync])
        residual(7)
        negate_mean(7)
        deviation(6)
        inverse_std(6)
        deviation(7)
        inverse_std(7)
        centre(6)
        centre(7)
        finish(6, [nc.sync])
        finish(7, [nc.sync, nc.scalar])
